import numpy as np
import ml_dtypes


def mxq(x, axis, fmt="e4m3"):
    dtype, down = {"e4m3": (ml_dtypes.float8_e4m3fn, 7), "e5m2": (ml_dtypes.float8_e5m2, 14)}[fmt]
    v = np.moveaxis(np.asarray(x, np.float32).astype(ml_dtypes.bfloat16).astype(np.float64), axis, -1)
    blocks = v.reshape(v.shape[:-1] + (-1, 32))
    amax = np.abs(blocks).max(-1, keepdims=True)
    byte = np.maximum(np.where(amax > 0, np.frexp(amax)[1] - 1 + 127, 0) - down, 1)
    scale = np.exp2(byte - 127.0)
    codes = (blocks / scale).astype(np.float32).astype(dtype).astype(np.float64)
    return np.moveaxis((codes * scale).reshape(v.shape), -1, axis)


WIDE = False


def mx_kscale(k):
    if not WIDE:
        return np.ones(k)
    levels = np.array([10, -10, 5, -5, 0])
    if k % 512:
        return np.exp2(np.random.permutation(np.resize(levels, k // 32))).repeat(32)
    a = np.empty((k // 512, 16))
    for p in range(k // 512):
        a[p, :8] = np.random.permutation(np.resize(levels, 8))
        for g in range(8):
            far = levels[np.abs(levels - a[p, g]) >= 10]
            a[p, g + 8] = far[np.random.randint(len(far))]
    return np.exp2(a.ravel()).repeat(32)


BF16 = ml_dtypes.bfloat16


def bf(x):
    return np.asarray(x, np.float32).astype(BF16)


def f64(x):
    return np.asarray(x).astype(np.float64)


B, N, E, H, G, C, EO = 1, 2048, 1024, 8, 128, 512, 1024
D = E // H
NB = N // C


def silu(v):
    return v / (1.0 + np.exp(-v))


def setup_inputs():
    s = mx_kscale(N)
    return {"q": bf(silu(0.4 * np.random.standard_normal((B, H, N, D)))),
            "k": bf(silu(0.4 * np.random.standard_normal((B, H, N, D))) * s[:, None]),
            "v": bf(silu(0.4 * np.random.standard_normal((B, H, N, D))) / s[:, None]),
            "log_slope": bf(-(3.0 + 5.0 * np.random.random(H)) / N)}


def reference(q, k, v, log_slope):
    ls = f64(log_slope)
    vq = mxq(f64(v), 2, "e4m3")
    idx = np.arange(N, dtype=np.float64)
    outs = []
    for i in range(NB):
        lo, hi = i * C, (i + 1) * C
        diff = idx[lo:hi, None] - idx[None, :hi]
        decay = np.where(diff >= 0, np.exp(ls[:, None, None] * np.maximum(diff, 0.0)), 0.0)
        energy = (f64(q)[:, :, lo:hi] @ f64(k)[:, :, :hi].transpose(0, 1, 3, 2)) * decay
        outs.append(mxq(energy, 3, "e4m3") @ vq[:, :, :hi])
    return np.concatenate(outs, axis=2)

@@ -1,0 +1,291 @@
+from contextlib import ExitStack
+
+import concourse.mybir as mybir
+from concourse.masks import make_identity
+
+F32 = mybir.dt.float32
+BF16 = mybir.dt.bfloat16
+I32 = mybir.dt.int32
+U32 = mybir.dt.uint32
+U8 = mybir.dt.uint8
+FP8X4 = mybir.dt.float8_e4m3fn_x4
+ALU = mybir.AluOpType
+ACT = mybir.ActivationFunctionType
+
+P = 128
+PACK = 4
+HEADS = 8
+SEQ = 2048
+HEAD_DIM = 128
+BLOCK = 512
+N_TILES = SEQ // P
+N_BLOCKS = SEQ // BLOCK
+TILES_PER_BLOCK = BLOCK // P
+UNITS_PER_HEAD = N_BLOCKS * (N_BLOCKS + 1) // 2
+FAR_STEPS = N_TILES - PACK
+FLIP_GROUPS = 2 * N_TILES // PACK
+FOREVER = 2.0**100
+TINY = 2.0**-60
+
+FLOPS = 2 * 2 * HEADS * HEAD_DIM * BLOCK * BLOCK * UNITS_PER_HEAD
+
+
+DIRECT = TILES_PER_BLOCK - 1
+HELPED = TILES_PER_BLOCK - 1
+RUN = 2
+
+
+def tile_tnlattention_pa_kernel(tc, q, k, v, log_slope, out):
+    nc = tc.nc
+    with ExitStack() as ctx:
+        const = ctx.enter_context(tc.tile_pool(name="const", bufs=1))
+        rows = ctx.enter_context(tc.tile_pool(name="rows", bufs=2))
+        head = ctx.enter_context(tc.tile_pool(name="head", bufs=2))
+        work = ctx.enter_context(tc.tile_pool(name="work", bufs=2))
+        psum_s = ctx.enter_context(tc.psum_pool(name="psum_s", bufs=5))
+        psum_o = ctx.enter_context(tc.psum_pool(name="psum_o", bufs=1))
+        psum_t = ctx.enter_context(tc.psum_pool(name="psum_t", bufs=2))
+        ctx.enter_context(tc.manual_schedule())
+
+        slope_bf = const.tile([P, HEADS], BF16)
+        nc.sync.dma_start(out=slope_bf[:], in_=log_slope.partition_broadcast(P))
+
+        ident = const.tile([P, P], BF16)
+        make_identity(nc, ident[:])
+
+        dist_int = const.tile([P, BLOCK, PACK], I32)
+        nc.gpsimd.iota(dist_int[:], pattern=[[1, BLOCK], [-1, PACK]], base=0, channel_multiplier=-PACK)
+        step_int = const.tile([P, FAR_STEPS], I32)
+        nc.gpsimd.iota(step_int[:], pattern=[[P, FAR_STEPS]], base=0, channel_multiplier=0)
+
+        dist = const.tile([P, BLOCK, PACK], F32)
+        nc.vector.tensor_copy(out=dist[:], in_=dist_int[:])
+        behind = const.tile([P, BLOCK, PACK], F32)
+        nc.vector.tensor_scalar(
+            out=behind[:], in0=dist[:], scalar1=0.0, scalar2=FOREVER, op0=ALU.is_lt, op1=ALU.mult
+        )
+        dist_causal = const.tile([P, BLOCK, PACK], F32)
+        nc.vector.tensor_tensor(out=dist_causal[:], in0=dist[:], in1=behind[:], op=ALU.add)
+        step = const.tile([P, FAR_STEPS], F32)
+        nc.vector.tensor_copy(out=step[:], in_=step_int[:])
+
+        slope = const.tile([P, HEADS], F32)
+        nc.vector.tensor_scalar_min(out=slope[:], in0=slope_bf[:], scalar1=-TINY)
+        slope_block = const.tile([P, HEADS], F32)
+        nc.vector.tensor_scalar_mul(out=slope_block[:], in0=slope[:], scalar1=float(BLOCK))
+
+        rows_of = {}
+        cols_of = {}
+        decay_of = {}
+        v_grouped_of = {}
+        v_of = {}
+        bank_of = {}
+        lifted_of = {}
+        direct_of = {}
+        helped_of = {}
+        codes_of = {}
+
+        def load(h):
+            kq_rows = rows.tile([P, 2, N_TILES, HEAD_DIM], BF16)
+            v_rows = rows.tile([P, N_TILES, HEAD_DIM], BF16)
+            nc.sync.dma_start(
+                out=kq_rows[:, 0].rearrange("p (g t) d -> p g t d", t=PACK),
+                in_=k[0, h].rearrange("(g p t) d -> p g t d", p=P, t=PACK),
+            )
+            nc.sync.dma_start(out=kq_rows[:, 1], in_=q[0, h].rearrange("(n p) d -> p n d", p=P))
+            nc.sync.dma_start(
+                out=v_rows[:].rearrange("p (g t) d -> p g t d", t=PACK),
+                in_=v[0, h].rearrange("(g p t) d -> p g t d", p=P, t=PACK),
+            )
+            rows_of[h] = (kq_rows, v_rows)
+
+        def prepare_step(h, u):
+            kq_rows, v_rows = rows_of[h]
+            slope_h = slope[:, h : h + 1]
+            if u == 0:
+                kq_cols = head.tile([P, 2 * SEQ], BF16)
+                cols_of[h] = kq_cols
+                far = head.tile([P, P, PACK], F32)
+                nc.scalar.activation(
+                    out=far[:], in_=dist[:, 0:P], func=ACT.Exp, bias=slope_block[:, h : h + 1], scale=slope_h
+                )
+                near = head.tile([P, BLOCK, PACK], F32)
+                nc.scalar.activation(out=near[:], in_=dist_causal[:], func=ACT.Exp, scale=slope_h)
+                far_step = head.tile([P, FAR_STEPS], F32)
+                nc.scalar.activation(out=far_step[:], in_=step[:], func=ACT.Exp, scale=slope_h)
+                decay_of[h] = (near, far, far_step)
+            if u < FLIP_GROUPS:
+                tiles = kq_rows[:].rearrange("p a n d -> p (a n) d")
+                flipped = psum_t.tile([P, PACK, P], BF16)
+                for j in range(PACK):
+                    nc.tensor.transpose(flipped[:, j, :], tiles[:, u * PACK + j, :], ident[:])
+                nc.scalar.copy(
+                    out=cols_of[h][:, u * BLOCK : (u + 1) * BLOCK],
+                    in_=flipped[:].rearrange("d j n -> d (j n)"),
+                )
+
+        def regroup_v(h, g):
+            kq_rows, v_rows = rows_of[h]
+            if g == 0:
+                v_grouped = head.tile([P, N_BLOCKS, HEAD_DIM, PACK], BF16, align_bytes=64)
+                v_grouped_of[h] = v_grouped
+            nc.scalar.copy(
+                out=v_grouped_of[h][:, g],
+                in_=v_rows[:, g * PACK : (g + 1) * PACK, :].rearrange("p t d -> p d t"),
+            )
+
+        def quantise_v(h):
+            v_codes = head.tile([P, N_BLOCKS * HEAD_DIM], U32, align_bytes=64)
+            v_scales = head.tile([P, N_BLOCKS * HEAD_DIM], U8, align_bytes=64)
+            nc.vector.quantize_mx(
+                out=v_codes[:].bitcast(FP8X4),
+                scales=v_scales[:],
+                in_=v_grouped_of[h][:].rearrange("p g d t -> p (g d t)"),
+            )
+            v_of[h] = (v_codes, v_scales)
+
+        units = [(h, b, g) for h in range(HEADS) for b in range(N_BLOCKS) for g in range(b + 1)]
+
+        def far_scalar(n, r):
+            h, b, g = units[n]
+            near, far, far_step = decay_of[h]
+            s = (b - g - 1) * TILES_PER_BLOCK + r
+            return far_step[:, s : s + 1]
+
+        def fill(n, r):
+            h, b, g = units[n]
+            kq_cols = cols_of[h]
+            q_tile = N_TILES + b * TILES_PER_BLOCK + r
+            s_bank = psum_s.tile([P, PACK, P], F32)
+            for t in range(PACK):
+                k_tile = g * PACK + t
+                nc.tensor.matmul(
+                    s_bank[:, t, :],
+                    lhsT=kq_cols[:, k_tile * P : (k_tile + 1) * P],
+                    rhs=kq_cols[:, q_tile * P : (q_tile + 1) * P],
+                    start=True,
+                    stop=True,
+                )
+            bank_of[(n, r)] = s_bank
+
+
+        def multiply(n, r):
+            h, b, g = units[n]
+            near, far, far_step = decay_of[h]
+            if r == 0:
+                direct = work.tile([P, DIRECT, P, PACK], BF16, align_bytes=64, bufs=RUN + 1)
+                direct_of[n] = direct
+            s_view = bank_of[(n, r)][:].rearrange("p t c -> p c t")
+            energy = direct_of[n][:, r]
+            if g == b:
+                nc.vector.tensor_tensor(out=energy, in0=s_view, in1=near[:, r * P : (r + 1) * P], op=ALU.mult)
+            else:
+                nc.vector.scalar_tensor_tensor(
+                    out=energy, in0=s_view, scalar=far_scalar(n, r), in1=far[:], op0=ALU.mult, op1=ALU.mult
+                )
+
+        def lift(n):
+            h, b, g = units[n]
+            s_view = bank_of[(n, HELPED)][:].rearrange("p t c -> p c t")
+            lifted = work.tile([P, P, PACK], F32, bufs=RUN + 2)
+            if g == b:
+                nc.scalar.copy(out=lifted[:], in_=s_view)
+            else:
+                nc.scalar.activation(out=lifted[:], in_=s_view, func=ACT.Copy, scale=far_scalar(n, HELPED))
+            lifted_of[n] = lifted
+
+        def help_multiply(n):
+            h, b, g = units[n]
+            near, far, far_step = decay_of[h]
+            helped = work.tile([P, P, PACK], BF16, align_bytes=64, bufs=RUN)
+            table = near[:, HELPED * P : (HELPED + 1) * P] if g == b else far[:]
+            nc.gpsimd.tensor_tensor(out=helped[:], in0=lifted_of[n][:], in1=table, op=ALU.mult)
+            helped_of[n] = helped
+
+        def quantise(energy, n, r):
+            h, b, g = units[n]
+            e_codes, e_scales = codes_of[(h, b)]
+            cols = slice(r * P, r * P + energy.shape[1] // PACK)
+            nc.vector.quantize_mx(out=e_codes[:, g, cols].bitcast(FP8X4), scales=e_scales[:, g, cols], in_=energy)
+
+        def quantise_run(first):
+            run = range(first, first + RUN)
+            for n in run:
+                h, b, g = units[n]
+                if n % UNITS_PER_HEAD == 0:
+                    quantise_v(h)
+                if g == 0:
+                    e_codes = work.tile([P, N_BLOCKS, BLOCK], U32, align_bytes=64)
+                    e_scales = work.tile([P, N_BLOCKS, BLOCK], U8, align_bytes=64)
+                    codes_of[(h, b)] = (e_codes, e_scales)
+                quantise(direct_of[n][:, 0:2].rearrange("p r c t -> p (r c t)"), n, 0)
+                quantise(direct_of[n][:, 2:3].rearrange("p r c t -> p (r c t)"), n, 2)
+            for n in run:
+                quantise(helped_of[n][:].rearrange("p c t -> p (c t)"), n, HELPED)
+
+        def second_matmul(h, b):
+            v_codes, v_scales = v_of[h]
+            e_codes, e_scales = codes_of[(h, b)]
+            o_bank = psum_o.tile([P, TILES_PER_BLOCK, HEAD_DIM], F32)
+            for r in range(TILES_PER_BLOCK):
+                q_cols = slice(r * P, (r + 1) * P)
+                for g in range(b + 1):
+                    v_cols = slice(g * HEAD_DIM, (g + 1) * HEAD_DIM)
+                    nc.tensor.matmul_mx(
+                        out=o_bank[:, r, :],
+                        lhsT=e_codes[:, g, q_cols].bitcast(FP8X4),
+                        lhsT_scale=e_scales[:, g, q_cols],
+                        rhs=v_codes[:, v_cols].bitcast(FP8X4),
+                        rhs_scale=v_scales[:, v_cols],
+                        start=(g == 0),
+                        stop=(g == b),
+                    )
+            o_rows = work.tile([P, TILES_PER_BLOCK, HEAD_DIM], F32)
+            nc.scalar.copy(out=o_rows[:], in_=o_bank[:])
+            nc.sync.dma_start(
+                out=out[0, h, b * BLOCK : (b + 1) * BLOCK, :].rearrange("(r p) d -> p r d", p=P),
+                in_=o_rows[:],
+            )
+
+        load(0)
+        load(1)
+        for u in range(FLIP_GROUPS):
+            prepare_step(0, u)
+        for early in range(RUN - 1):
+            fill(early, HELPED)
+            lift(early)
+        for g in range(N_BLOCKS):
+            regroup_v(0, g)
+        for n in range(len(units) + 2):
+            filling = n < len(units)
+            multiplying = 1 <= n <= len(units)
+            turn = n % RUN == 1
+            if filling:
+                if n % UNITS_PER_HEAD == 0 and n // UNITS_PER_HEAD + 2 < HEADS:
+                    load(n // UNITS_PER_HEAD + 2)
+                fill(n, 0)
+                fill(n, 1)
+            if multiplying:
+                multiply(n - 1, 0)
+            if turn and n > RUN:
+                quantise_run(n - 1 - RUN)
+            if turn and filling:
+                for later in range(n - 1, n - 1 + RUN):
+                    help_multiply(later)
+            if filling:
+                fill(n, 2)
+            if multiplying:
+                multiply(n - 1, 1)
+                multiply(n - 1, 2)
+            if n + RUN - 1 < len(units):
+                fill(n + RUN - 1, HELPED)
+                lift(n + RUN - 1)
+            if filling and n // UNITS_PER_HEAD + 1 < HEADS and n % UNITS_PER_HEAD < FLIP_GROUPS:
+                prepare_step(n // UNITS_PER_HEAD + 1, n % UNITS_PER_HEAD)
+                if n % UNITS_PER_HEAD < N_BLOCKS:
+                    regroup_v(n // UNITS_PER_HEAD + 1, n % UNITS_PER_HEAD)
+            if turn and n > RUN:
+                for done in range(n - 1 - RUN, n - 1):
+                    h, b, g = units[done]
+                    if g == b:
+                        second_matmul(h, b)

@@ -18,21 +18,47 @@ HEADS = 8
 SEQ = 2048
 HEAD_DIM = 128
 BLOCK = 512
-N_TILES = SEQ // P
 N_BLOCKS = SEQ // BLOCK
 TILES_PER_BLOCK = BLOCK // P
-UNITS_PER_HEAD = N_BLOCKS * (N_BLOCKS + 1) // 2
-FAR_STEPS = N_TILES - PACK
-FLIP_GROUPS = 2 * N_TILES // PACK
+N_PAIRS = N_BLOCKS // 2
+LAST = TILES_PER_BLOCK - 1
+STEP = P // PACK
+FAR_STEPS = (N_BLOCKS - 1) * TILES_PER_BLOCK
 FOREVER = 2.0**100
 TINY = 2.0**-60
 
-FLOPS = 2 * 2 * HEADS * HEAD_DIM * BLOCK * BLOCK * UNITS_PER_HEAD
+FLOPS = 2 * 2 * HEADS * HEAD_DIM * BLOCK * BLOCK * (N_BLOCKS * (N_BLOCKS + 1) // 2)
+
+CYCLE = 17
+HELP = 5
+DIRECT = CYCLE - HELP
+BANKS = 4
+
+FIRST = (
+    [("far", 1, 0, r) for r in range(TILES_PER_BLOCK)]
+    + [("near", 0), ("near", 1)]
+    + [("far", 2, g, r) for g in range(2) for r in range(TILES_PER_BLOCK)]
+    + [("pack", 0, r) for r in range(LAST)]
+)
+SECOND = (
+    [("near", 2), ("near", 3)]
+    + [("far", 3, g, r) for g in range(3) for r in range(TILES_PER_BLOCK)]
+    + [("pack", 1, r) for r in range(LAST)]
+)
+HALVES = [FIRST, SECOND]
+HELPED_AT = [[3, 6, 8, 10, 12], [3, 5, 7, 9, 11]]
 
 
-DIRECT = TILES_PER_BLOCK - 1
-HELPED = TILES_PER_BLOCK - 1
-RUN = 2
+def widths(n):
+    runs = []
+    at = 0
+    while at < n:
+        w = 8
+        while w > n - at:
+            w //= 2
+        runs.append((at, w))
+        at += w
+    return runs
 
 
 def tile_tnlattention_pa_kernel(tc, q, k, v, log_slope, out):
@@ -42,203 +68,312 @@ def tile_tnlattention_pa_kernel(tc, q, k, v, log_slope, out):
         rows = ctx.enter_context(tc.tile_pool(name="rows", bufs=2))
         head = ctx.enter_context(tc.tile_pool(name="head", bufs=2))
         work = ctx.enter_context(tc.tile_pool(name="work", bufs=2))
-        psum_s = ctx.enter_context(tc.psum_pool(name="psum_s", bufs=5))
+        psum_s = ctx.enter_context(tc.psum_pool(name="psum_s", bufs=BANKS))
+        psum_l = ctx.enter_context(tc.psum_pool(name="psum_l", bufs=2))
         psum_o = ctx.enter_context(tc.psum_pool(name="psum_o", bufs=1))
-        psum_t = ctx.enter_context(tc.psum_pool(name="psum_t", bufs=2))
+        psum_t = ctx.enter_context(tc.psum_pool(name="psum_t", bufs=1))
         ctx.enter_context(tc.manual_schedule())
+
+        rows_of = {}
+
+        def load(h, split):
+            k_rows = rows.tile([P, N_BLOCKS, PACK, HEAD_DIM], BF16)
+            q_rows = rows.tile([P, N_BLOCKS, TILES_PER_BLOCK, HEAD_DIM], BF16)
+            v_rows = rows.tile([P, N_BLOCKS, PACK, HEAD_DIM], BF16)
+            k_src = k[0, h].rearrange("(g p t) d -> p g t d", p=P, t=PACK)
+            v_src = v[0, h].rearrange("(g p t) d -> p g t d", p=P, t=PACK)
+            q_src = q[0, h].rearrange("(b r p) d -> p b r d", p=P, r=TILES_PER_BLOCK)
+            for lo, hi in split:
+                nc.sync.dma_start(out=k_rows[:, lo:hi], in_=k_src[:, lo:hi])
+                nc.sync.dma_start(out=q_rows[:, lo:hi], in_=q_src[:, lo:hi])
+            nc.sync.dma_start(out=v_rows[:], in_=v_src)
+            rows_of[h] = (k_rows, q_rows, v_rows)
 
         slope_bf = const.tile([P, HEADS], BF16)
         nc.sync.dma_start(out=slope_bf[:], in_=log_slope.partition_broadcast(P))
+        load(0, [(0, 1), (1, 2), (2, N_BLOCKS)])
+        load(1, [(0, N_BLOCKS)])
 
         ident = const.tile([P, P], BF16)
         make_identity(nc, ident[:])
 
-        dist_int = const.tile([P, BLOCK, PACK], I32)
-        nc.gpsimd.iota(dist_int[:], pattern=[[1, BLOCK], [-1, PACK]], base=0, channel_multiplier=-PACK)
+        dist_int = const.tile([P, P, PACK], I32)
+        nc.gpsimd.iota(dist_int[:], pattern=[[1, P], [-1, PACK]], base=LAST * P, channel_multiplier=-PACK)
         step_int = const.tile([P, FAR_STEPS], I32)
         nc.gpsimd.iota(step_int[:], pattern=[[P, FAR_STEPS]], base=0, channel_multiplier=0)
 
-        dist = const.tile([P, BLOCK, PACK], F32)
-        nc.vector.tensor_copy(out=dist[:], in_=dist_int[:])
-        behind = const.tile([P, BLOCK, PACK], F32)
-        nc.vector.tensor_scalar(
-            out=behind[:], in0=dist[:], scalar1=0.0, scalar2=FOREVER, op0=ALU.is_lt, op1=ALU.mult
-        )
-        dist_causal = const.tile([P, BLOCK, PACK], F32)
-        nc.vector.tensor_tensor(out=dist_causal[:], in0=dist[:], in1=behind[:], op=ALU.add)
-        step = const.tile([P, FAR_STEPS], F32)
-        nc.vector.tensor_copy(out=step[:], in_=step_int[:])
+        k_even_a = const.tile([P, N_PAIRS, PACK, LAST * STEP + P], BF16, align_bytes=64)
+        k_even_b = const.tile([P, N_PAIRS, PACK, LAST * STEP + P], BF16, align_bytes=64)
+        k_part_a = const.tile([P, LAST, N_PAIRS, PACK, P], BF16, align_bytes=64)
+        k_part_b = const.tile([P, LAST, N_PAIRS, PACK, P], BF16, align_bytes=64)
+        v_part_a = const.tile([P, 2, LAST, N_PAIRS, HEAD_DIM], U32, align_bytes=64)
+        v_part_b = const.tile([P, 2, LAST, N_PAIRS, HEAD_DIM], U32, align_bytes=64)
+        vs_part_a = const.tile([P, LAST, N_PAIRS, HEAD_DIM], U8, align_bytes=64)
+        vs_part_b = const.tile([P, LAST, N_PAIRS, HEAD_DIM], U8, align_bytes=64)
+        v_scales_a = const.tile([P, N_BLOCKS, HEAD_DIM], U8, align_bytes=64)
+        v_scales_b = const.tile([P, N_BLOCKS, HEAD_DIM], U8, align_bytes=64)
+        k_even = [k_even_a, k_even_b]
+        k_part = [k_part_a, k_part_b]
+        v_part = [v_part_a, v_part_b]
+        vs_part = [vs_part_a, vs_part_b]
+        v_scales = [v_scales_a, v_scales_b]
+
+        def zero_set(i):
+            nc.gpsimd.memset(k_even[i][:].bitcast(U32)[:, :, :, 0 : LAST * STEP // 2], 0)
+            for r in range(LAST):
+                nc.gpsimd.memset(k_part[i][:].bitcast(U32)[:, r, :, :, (r + 1) * STEP // 2 : P // 2], 0)
+            nc.gpsimd.memset(v_part[i][:], 0)
+            nc.gpsimd.memset(vs_part[i][:].bitcast(U32), 0)
+            nc.gpsimd.memset(v_scales[i][:].bitcast(U32), 0)
+
+        zero_set(0)
 
         slope = const.tile([P, HEADS], F32)
         nc.vector.tensor_scalar_min(out=slope[:], in0=slope_bf[:], scalar1=-TINY)
-        slope_block = const.tile([P, HEADS], F32)
-        nc.vector.tensor_scalar_mul(out=slope_block[:], in0=slope[:], scalar1=float(BLOCK))
+        slope_tile = const.tile([P, HEADS], F32)
+        nc.vector.tensor_scalar_mul(out=slope_tile[:], in0=slope[:], scalar1=float(P))
+        dist = const.tile([P, P, PACK], F32)
+        nc.vector.tensor_copy(out=dist[:], in_=dist_int[:])
+        step = const.tile([P, FAR_STEPS], F32)
+        nc.vector.tensor_copy(out=step[:], in_=step_int[:])
+        causal = const.tile([P, 1 + LAST, P, PACK], F32)
+        nc.vector.scalar_tensor_tensor(
+            out=causal[:, LAST], in0=dist[:], scalar=-FOREVER, in1=dist[:], op0=ALU.mult, op1=ALU.max
+        )
+        shift = const.tile([P, LAST], F32)
+        nc.vector.memset(shift[:], 0.0)
+        for r in range(LAST):
+            nc.vector.memset(shift[0 : (LAST - r) * STEP, r : r + 1], -float(P * (1 + r)))
+            moved = const.tile([P, P, PACK], F32)
+            nc.vector.tensor_scalar_add(out=moved[:], in0=dist[:], scalar1=shift[:, r : r + 1])
+            nc.vector.scalar_tensor_tensor(
+                out=causal[:, r], in0=moved[:], scalar=-FOREVER, in1=moved[:], op0=ALU.mult, op1=ALU.max
+            )
 
-        rows_of = {}
-        cols_of = {}
-        decay_of = {}
+        q_cols_of = {}
+        k_odd_of = {}
+        table_of = {}
+        far_step_of = {}
         v_grouped_of = {}
-        v_of = {}
-        bank_of = {}
-        lifted_of = {}
-        direct_of = {}
-        helped_of = {}
-        codes_of = {}
+        v_codes_of = {}
 
-        def load(h):
-            kq_rows = rows.tile([P, 2, N_TILES, HEAD_DIM], BF16)
-            v_rows = rows.tile([P, N_TILES, HEAD_DIM], BF16)
-            nc.sync.dma_start(
-                out=kq_rows[:, 0].rearrange("p (g t) d -> p g t d", t=PACK),
-                in_=k[0, h].rearrange("(g p t) d -> p g t d", p=P, t=PACK),
-            )
-            nc.sync.dma_start(out=kq_rows[:, 1], in_=q[0, h].rearrange("(n p) d -> p n d", p=P))
-            nc.sync.dma_start(
-                out=v_rows[:].rearrange("p (g t) d -> p g t d", t=PACK),
-                in_=v[0, h].rearrange("(g p t) d -> p g t d", p=P, t=PACK),
-            )
-            rows_of[h] = (kq_rows, v_rows)
+        def flip(tiles):
+            flipped = psum_t.tile([P, PACK, P], BF16)
+            for j in range(PACK):
+                nc.tensor.transpose(flipped[:, j, :], tiles[:, j, :], ident[:])
+            return flipped
 
-        def prepare_step(h, u):
-            kq_rows, v_rows = rows_of[h]
+        def flip_q(h, b):
+            if h not in q_cols_of:
+                q_cols = head.tile([P, N_BLOCKS, TILES_PER_BLOCK, P], BF16)
+                q_cols_of[h] = q_cols
+            nc.scalar.copy(out=q_cols_of[h][:, b], in_=flip(rows_of[h][1][:, b])[:])
+
+        def flip_k(h, g):
+            if h not in k_odd_of:
+                k_odd = head.tile([P, N_PAIRS, PACK, P], BF16, align_bytes=64)
+                k_odd_of[h] = k_odd
+            flipped = flip(rows_of[h][0][:, g])
+            if g % 2 == 0:
+                nc.scalar.copy(out=k_even[h % 2][:, g // 2, :, LAST * STEP :], in_=flipped[:])
+            else:
+                nc.scalar.copy(out=k_odd_of[h][:, g // 2], in_=flipped[:])
+                for r in range(LAST):
+                    nc.sync.dma_start(
+                        out=k_part[h % 2][:, r, g // 2, :, 0 : (r + 1) * STEP],
+                        in_=k_odd_of[h][:, g // 2, :, 0 : (r + 1) * STEP],
+                    )
+
+        def decay(h, which):
             slope_h = slope[:, h : h + 1]
-            if u == 0:
-                kq_cols = head.tile([P, 2 * SEQ], BF16)
-                cols_of[h] = kq_cols
+            if which == "far":
                 far = head.tile([P, P, PACK], F32)
                 nc.scalar.activation(
-                    out=far[:], in_=dist[:, 0:P], func=ACT.Exp, bias=slope_block[:, h : h + 1], scale=slope_h
+                    out=far[:], in_=dist[:], func=ACT.Exp, bias=slope_tile[:, h : h + 1], scale=slope_h
                 )
-                near = head.tile([P, BLOCK, PACK], F32)
-                nc.scalar.activation(out=near[:], in_=dist_causal[:], func=ACT.Exp, scale=slope_h)
+                table_of[(h, "far")] = far
                 far_step = head.tile([P, FAR_STEPS], F32)
                 nc.scalar.activation(out=far_step[:], in_=step[:], func=ACT.Exp, scale=slope_h)
-                decay_of[h] = (near, far, far_step)
-            if u < FLIP_GROUPS:
-                tiles = kq_rows[:].rearrange("p a n d -> p (a n) d")
-                flipped = psum_t.tile([P, PACK, P], BF16)
-                for j in range(PACK):
-                    nc.tensor.transpose(flipped[:, j, :], tiles[:, u * PACK + j, :], ident[:])
-                nc.scalar.copy(
-                    out=cols_of[h][:, u * BLOCK : (u + 1) * BLOCK],
-                    in_=flipped[:].rearrange("d j n -> d (j n)"),
-                )
+                far_step_of[h] = far_step
+            else:
+                near = head.tile([P, P, PACK], F32, bufs=2 * (1 + LAST))
+                nc.scalar.activation(out=near[:], in_=causal[:, which], func=ACT.Exp, scale=slope_h)
+                table_of[(h, which)] = near
 
         def regroup_v(h, g):
-            kq_rows, v_rows = rows_of[h]
             if g == 0:
                 v_grouped = head.tile([P, N_BLOCKS, HEAD_DIM, PACK], BF16, align_bytes=64)
                 v_grouped_of[h] = v_grouped
-            nc.scalar.copy(
-                out=v_grouped_of[h][:, g],
-                in_=v_rows[:, g * PACK : (g + 1) * PACK, :].rearrange("p t d -> p d t"),
-            )
+            nc.scalar.copy(out=v_grouped_of[h][:, g], in_=rows_of[h][2][:, g].rearrange("p t d -> p d t"))
 
         def quantise_v(h):
-            v_codes = head.tile([P, N_BLOCKS * HEAD_DIM], U32, align_bytes=64)
-            v_scales = head.tile([P, N_BLOCKS * HEAD_DIM], U8, align_bytes=64)
+            v_codes = head.tile([P, N_BLOCKS, HEAD_DIM], U32, align_bytes=64)
             nc.vector.quantize_mx(
-                out=v_codes[:].bitcast(FP8X4),
-                scales=v_scales[:],
+                out=v_codes[:].rearrange("p g d -> p (g d)").bitcast(FP8X4),
+                scales=v_scales[h % 2][:].rearrange("p g d -> p (g d)"),
                 in_=v_grouped_of[h][:].rearrange("p g d t -> p (g d t)"),
             )
-            v_of[h] = (v_codes, v_scales)
+            v_codes_of[h] = v_codes
 
-        units = [(h, b, g) for h in range(HEADS) for b in range(N_BLOCKS) for g in range(b + 1)]
+        def spread_v(h):
+            v_codes = v_codes_of[h]
+            for r in range(LAST):
+                live = (r + 1) * STEP
+                even_words = v_codes[0:live].rearrange("p (j e) d -> p e j d", e=2)
+                even_scales = v_scales[h % 2][0:live].rearrange("p (j e) d -> p e j d", e=2)
+                nc.sync.dma_start(
+                    out=v_part[h % 2][P - live : P, 0, r].bitcast(I32), in_=even_words[:, 0].bitcast(I32)
+                )
+                nc.sync.dma_start(
+                    out=vs_part[h % 2][P - live : P, r].bitcast(I32), in_=even_scales[:, 0].bitcast(I32)
+                )
+                nc.sync.dma_start(
+                    out=v_part[h % 2][0:live, 1, r].bitcast(I32), in_=even_words[:, 1].bitcast(I32)
+                )
 
-        def far_scalar(n, r):
-            h, b, g = units[n]
-            near, far, far_step = decay_of[h]
+        halves = [(h, i) for h in range(HEADS) for i in range(2)]
+        direct_tiles = []
+        helped_tiles = []
+        place = {}
+        for c, (h, i) in enumerate(halves):
+            helped = []
+            direct = 0
+            for at, tile in enumerate(HALVES[i]):
+                if at in HELPED_AT[i]:
+                    slot = DIRECT + len(helped)
+                    helped.append((slot, h, tile))
+                else:
+                    slot = direct
+                    direct_tiles.append((c, slot, h, tile))
+                    direct += 1
+                place[(h, tile)] = (c, slot)
+            helped_tiles.append(helped)
+
+        def product(bank, h, tile):
+            def k_cols(g, t):
+                if g % 2 == 0:
+                    return k_even[h % 2][:, g // 2, t, LAST * STEP :]
+                return k_odd_of[h][:, g // 2, t]
+
+            q_cols = q_cols_of[h]
+            if tile[0] == "pack":
+                kind, j, r = tile
+                for t in range(PACK):
+                    nc.tensor.matmul(
+                        bank[:, t, :],
+                        lhsT=k_even[h % 2][:, j, t, r * STEP : r * STEP + P],
+                        rhs=q_cols[:, 2 * j, r],
+                        start=True,
+                        stop=False,
+                    )
+                    nc.tensor.matmul(
+                        bank[:, t, :],
+                        lhsT=k_part[h % 2][:, LAST - 1 - r, j, t],
+                        rhs=q_cols[:, 2 * j + 1, LAST - 1 - r],
+                        start=False,
+                        stop=True,
+                    )
+            else:
+                b = tile[1]
+                g, r = (b, LAST) if tile[0] == "near" else tile[2:]
+                for t in range(PACK):
+                    nc.tensor.matmul(bank[:, t, :], lhsT=k_cols(g, t), rhs=q_cols[:, b, r], start=True, stop=True)
+
+        def far_scalar(h, tile):
+            kind, b, g, r = tile
             s = (b - g - 1) * TILES_PER_BLOCK + r
-            return far_step[:, s : s + 1]
+            return far_step_of[h][:, s : s + 1]
 
-        def fill(n, r):
-            h, b, g = units[n]
-            kq_cols = cols_of[h]
-            q_tile = N_TILES + b * TILES_PER_BLOCK + r
+        def table(h, tile):
+            if tile[0] == "far":
+                return table_of[(h, "far")]
+            return table_of[(h, LAST if tile[0] == "near" else tile[2])]
+
+        bank_of = {}
+        energy_of = {}
+        helped_of = {}
+        lifted_of = {}
+        codes_of = {}
+
+        def fill(n):
+            c, slot, h, tile = direct_tiles[n]
             s_bank = psum_s.tile([P, PACK, P], F32)
-            for t in range(PACK):
-                k_tile = g * PACK + t
-                nc.tensor.matmul(
-                    s_bank[:, t, :],
-                    lhsT=kq_cols[:, k_tile * P : (k_tile + 1) * P],
-                    rhs=kq_cols[:, q_tile * P : (q_tile + 1) * P],
-                    start=True,
-                    stop=True,
-                )
-            bank_of[(n, r)] = s_bank
+            product(s_bank, h, tile)
+            bank_of[n] = s_bank
 
 
-        def multiply(n, r):
-            h, b, g = units[n]
-            near, far, far_step = decay_of[h]
-            if r == 0:
-                direct = work.tile([P, DIRECT, P, PACK], BF16, align_bytes=64, bufs=RUN + 1)
-                direct_of[n] = direct
-            s_view = bank_of[(n, r)][:].rearrange("p t c -> p c t")
-            energy = direct_of[n][:, r]
-            if g == b:
-                nc.vector.tensor_tensor(out=energy, in0=s_view, in1=near[:, r * P : (r + 1) * P], op=ALU.mult)
-            else:
+        def multiply(n):
+            c, slot, h, tile = direct_tiles[n]
+            if slot == 0:
+                energy = work.tile([P, DIRECT, P, PACK], BF16, align_bytes=64)
+                energy_of[c] = energy
+            s_view = bank_of[n][:].rearrange("p t c -> p c t")
+            dst = energy_of[c][:, slot]
+            if tile[0] == "far":
                 nc.vector.scalar_tensor_tensor(
-                    out=energy, in0=s_view, scalar=far_scalar(n, r), in1=far[:], op0=ALU.mult, op1=ALU.mult
+                    out=dst, in0=s_view, scalar=far_scalar(h, tile), in1=table(h, tile)[:], op0=ALU.mult, op1=ALU.mult
                 )
-
-        def lift(n):
-            h, b, g = units[n]
-            s_view = bank_of[(n, HELPED)][:].rearrange("p t c -> p c t")
-            lifted = work.tile([P, P, PACK], F32, bufs=RUN + 2)
-            if g == b:
-                nc.scalar.copy(out=lifted[:], in_=s_view)
             else:
-                nc.scalar.activation(out=lifted[:], in_=s_view, func=ACT.Copy, scale=far_scalar(n, HELPED))
-            lifted_of[n] = lifted
+                nc.vector.tensor_tensor(out=dst, in0=s_view, in1=table(h, tile)[:], op=ALU.mult)
 
-        def help_multiply(n):
-            h, b, g = units[n]
-            near, far, far_step = decay_of[h]
-            helped = work.tile([P, P, PACK], BF16, align_bytes=64, bufs=RUN)
-            table = near[:, HELPED * P : (HELPED + 1) * P] if g == b else far[:]
-            nc.gpsimd.tensor_tensor(out=helped[:], in0=lifted_of[n][:], in1=table, op=ALU.mult)
-            helped_of[n] = helped
+        def lift(c, i):
+            slot, h, tile = helped_tiles[c][i]
+            l_bank = psum_l.tile([P, PACK, P], F32)
+            product(l_bank, h, tile)
+            s_view = l_bank[:].rearrange("p t c -> p c t")
+            lifted = work.tile([P, P, PACK], F32, bufs=2 * HELP)
+            if tile[0] == "far":
+                nc.scalar.activation(out=lifted[:], in_=s_view, func=ACT.Copy, scale=far_scalar(h, tile))
+            else:
+                nc.scalar.copy(out=lifted[:], in_=s_view)
+            lifted_of[(c, i)] = lifted
 
-        def quantise(energy, n, r):
-            h, b, g = units[n]
-            e_codes, e_scales = codes_of[(h, b)]
-            cols = slice(r * P, r * P + energy.shape[1] // PACK)
-            nc.vector.quantize_mx(out=e_codes[:, g, cols].bitcast(FP8X4), scales=e_scales[:, g, cols], in_=energy)
+        def help_multiply(c, i):
+            slot, h, tile = helped_tiles[c][i]
+            if i == 0:
+                helped = work.tile([P, HELP, P, PACK], BF16, align_bytes=64, bufs=1)
+                helped_of[c] = helped
+            nc.gpsimd.tensor_tensor(
+                out=helped_of[c][:, i], in0=lifted_of[(c, i)][:], in1=table(h, tile)[:], op=ALU.mult
+            )
 
-        def quantise_run(first):
-            run = range(first, first + RUN)
-            for n in run:
-                h, b, g = units[n]
-                if n % UNITS_PER_HEAD == 0:
-                    quantise_v(h)
-                if g == 0:
-                    e_codes = work.tile([P, N_BLOCKS, BLOCK], U32, align_bytes=64)
-                    e_scales = work.tile([P, N_BLOCKS, BLOCK], U8, align_bytes=64)
-                    codes_of[(h, b)] = (e_codes, e_scales)
-                quantise(direct_of[n][:, 0:2].rearrange("p r c t -> p (r c t)"), n, 0)
-                quantise(direct_of[n][:, 2:3].rearrange("p r c t -> p (r c t)"), n, 2)
-            for n in run:
-                quantise(helped_of[n][:].rearrange("p c t -> p (c t)"), n, HELPED)
+        def quantise(c):
+            e_codes = work.tile([P, CYCLE, P], U32, align_bytes=64, bufs=3)
+            e_scales = work.tile([P, CYCLE, P], U8, align_bytes=64, bufs=3)
+            codes_of[c] = (e_codes, e_scales)
+            for source, base, n in ((energy_of[c], 0, DIRECT), (helped_of[c], DIRECT, HELP)):
+                for at, w in widths(n):
+                    slots = slice(base + at, base + at + w)
+                    nc.vector.quantize_mx(
+                        out=e_codes[:, slots].rearrange("p s c -> p (s c)").bitcast(FP8X4),
+                        scales=e_scales[:, slots].rearrange("p s c -> p (s c)"),
+                        in_=source[:, at : at + w].rearrange("p s c t -> p (s c t)"),
+                    )
 
         def second_matmul(h, b):
-            v_codes, v_scales = v_of[h]
-            e_codes, e_scales = codes_of[(h, b)]
             o_bank = psum_o.tile([P, TILES_PER_BLOCK, HEAD_DIM], F32)
             for r in range(TILES_PER_BLOCK):
-                q_cols = slice(r * P, (r + 1) * P)
-                for g in range(b + 1):
-                    v_cols = slice(g * HEAD_DIM, (g + 1) * HEAD_DIM)
+                passes = []
+                for g in range(b):
+                    passes.append((("far", b, g, r), v_codes_of[h][:, g], v_scales[h % 2][:, g]))
+                j, odd = b // 2, b % 2
+                if r == LAST:
+                    passes.append((("near", b), v_codes_of[h][:, b], v_scales[h % 2][:, b]))
+                elif odd:
+                    passes.append((("pack", j, LAST - 1 - r), v_part[h % 2][:, 1, r, j], v_scales[h % 2][:, b]))
+                else:
+                    passes.append((("pack", j, r), v_part[h % 2][:, 0, r, j], vs_part[h % 2][:, r, j]))
+                for i, (tile, v_words, v_sc) in enumerate(passes):
+                    c, slot = place[(h, tile)]
+                    e_codes, e_scales = codes_of[c]
                     nc.tensor.matmul_mx(
                         out=o_bank[:, r, :],
-                        lhsT=e_codes[:, g, q_cols].bitcast(FP8X4),
-                        lhsT_scale=e_scales[:, g, q_cols],
-                        rhs=v_codes[:, v_cols].bitcast(FP8X4),
-                        rhs_scale=v_scales[:, v_cols],
-                        start=(g == 0),
-                        stop=(g == b),
+                        lhsT=e_codes[:, slot].bitcast(FP8X4),
+                        lhsT_scale=e_scales[:, slot],
+                        rhs=v_words.bitcast(FP8X4),
+                        rhs_scale=v_sc,
+                        start=(i == 0),
+                        stop=(i == len(passes) - 1),
                     )
             o_rows = work.tile([P, TILES_PER_BLOCK, HEAD_DIM], F32)
             nc.scalar.copy(out=o_rows[:], in_=o_bank[:])
@@ -247,45 +382,91 @@ def tile_tnlattention_pa_kernel(tc, q, k, v, log_slope, out):
                 in_=o_rows[:],
             )
 
-        load(0)
-        load(1)
-        for u in range(FLIP_GROUPS):
-            prepare_step(0, u)
-        for early in range(RUN - 1):
-            fill(early, HELPED)
-            lift(early)
-        for g in range(N_BLOCKS):
-            regroup_v(0, g)
-        for n in range(len(units) + 2):
-            filling = n < len(units)
-            multiplying = 1 <= n <= len(units)
-            turn = n % RUN == 1
-            if filling:
-                if n % UNITS_PER_HEAD == 0 and n // UNITS_PER_HEAD + 2 < HEADS:
-                    load(n // UNITS_PER_HEAD + 2)
-                fill(n, 0)
-                fill(n, 1)
-            if multiplying:
-                multiply(n - 1, 0)
-            if turn and n > RUN:
-                quantise_run(n - 1 - RUN)
-            if turn and filling:
-                for later in range(n - 1, n - 1 + RUN):
-                    help_multiply(later)
-            if filling:
-                fill(n, 2)
-            if multiplying:
-                multiply(n - 1, 1)
-                multiply(n - 1, 2)
-            if n + RUN - 1 < len(units):
-                fill(n + RUN - 1, HELPED)
-                lift(n + RUN - 1)
-            if filling and n // UNITS_PER_HEAD + 1 < HEADS and n % UNITS_PER_HEAD < FLIP_GROUPS:
-                prepare_step(n // UNITS_PER_HEAD + 1, n % UNITS_PER_HEAD)
-                if n % UNITS_PER_HEAD < N_BLOCKS:
-                    regroup_v(n // UNITS_PER_HEAD + 1, n % UNITS_PER_HEAD)
-            if turn and n > RUN:
-                for done in range(n - 1 - RUN, n - 1):
-                    h, b, g = units[done]
-                    if g == b:
-                        second_matmul(h, b)
+        def chore(c, s):
+            h, i = halves[c]
+            nxt = h + 1 if h + 1 < HEADS else None
+            if i == 0:
+                if s == 0 and h + 2 < HEADS:
+                    load(h + 2, [(0, N_BLOCKS)])
+                if s == 0 and h > 0:
+                    second_matmul(h - 1, 2)
+                if s == 4 and h > 0:
+                    second_matmul(h - 1, 3)
+            else:
+                if s == 0:
+                    second_matmul(h, 0)
+                if s == 3:
+                    second_matmul(h, 1)
+            if nxt is None:
+                return
+            if i == 0:
+                if s in (1, 3, 5, 7):
+                    flip_k(nxt, s // 2)
+                if s in (9, 11):
+                    flip_q(nxt, (s - 7) // 2)
+                if s == 2:
+                    decay(nxt, "far")
+                if s in (6, 8, 10):
+                    decay(nxt, (LAST, 0, 1)[s // 2 - 3])
+            else:
+                if s in (1, 2, 4, 5):
+                    regroup_v(nxt, (1, 2, 4, 5).index(s))
+                if s == 6:
+                    flip_q(nxt, 0)
+                if s == 8:
+                    flip_q(nxt, 3)
+                if s == 10:
+                    decay(nxt, 2)
+
+        flip_k(0, 0)
+        flip_q(0, 1)
+        decay(0, "far")
+        fill(0)
+        fill(1)
+        lift(0, 0)
+        fill(2)
+        flip_q(0, 0)
+        flip_k(0, 1)
+        decay(0, LAST)
+        fill(3)
+        help_multiply(0, 0)
+        flip_q(0, 2)
+        flip_q(0, 3)
+        n = 0
+        for c in range(len(halves)):
+            for s in range(DIRECT):
+                multiply(n)
+                if n + BANKS < len(direct_tiles):
+                    fill(n + BANKS)
+                if c == 0:
+                    if s in (0, 2, 4, 6):
+                        lift(0, s // 2 + 1)
+                        help_multiply(0, s // 2 + 1)
+                    if s == 1:
+                        flip_k(0, 2)
+                    if s == 3:
+                        flip_k(0, 3)
+                    if s in (5, 6, 7):
+                        decay(0, s - 5)
+                    if s in (7, 8, 9, 10):
+                        regroup_v(0, s - 7)
+                chore(c, s)
+                n += 1
+            if c + 1 < len(halves):
+                for i in range(HELP):
+                    lift(c + 1, i)
+            h, i = halves[c]
+            if c == 0:
+                quantise_v(0)
+                spread_v(0)
+            if i == 1 and h + 1 < HEADS:
+                quantise_v(h + 1)
+                spread_v(h + 1)
+            quantise(c)
+            if c + 1 < len(halves):
+                for i in range(HELP):
+                    help_multiply(c + 1, i)
+            if c == 0:
+                zero_set(1)
+        second_matmul(HEADS - 1, 2)
+        second_matmul(HEADS - 1, 3)

@@ -32,21 +32,50 @@ FLOPS = 2 * 2 * HEADS * HEAD_DIM * BLOCK * BLOCK * (N_BLOCKS * (N_BLOCKS + 1) //
 CYCLE = 17
 HELP = 5
 DIRECT = CYCLE - HELP
+A_MX2 = (0, 1, 2, 3)
+A_O2 = 4
+A_MX3 = (6, 7, 8, 9)
+A_O3 = 11
+A_OWN = ((0, "v", 2), (2, "v", 3))
+A_PREP = ((3, "k", 0), (5, "k", 1), (7, "q", 1), (8, "q", 2), (9, "far", 0))
+B_MX0 = (4, 5)
+B_O0 = 6
+B_MX1 = (7, 8, 9, 10)
+B_O1 = 11
+B_PREP = ((0, "q", 0), (2, "k", 2), (3, "k", 3), (4, "near", 0), (8, "q", 3), (9, "v", 0), (10, "v", 1))
+LIFT_AT = ((1, 3, 6, 8), (1, 3, 6, 8))
+LIFT_0 = (4, 5, 6, 8)
+START_LIFT = (0, 1, 2, 3)
+START_PREP = ((0, "q", 3), (2, "k", 2), (4, "k", 3), (6, "v", 0), (7, "v", 1), (8, "v", 2), (9, "v", 3))
 BANKS = 4
 
-FIRST = (
+OPENING = (
     [("far", 1, 0, r) for r in range(TILES_PER_BLOCK)]
     + [("near", 0), ("near", 1)]
     + [("far", 2, g, r) for g in range(2) for r in range(TILES_PER_BLOCK)]
     + [("pack", 0, r) for r in range(LAST)]
 )
-SECOND = (
-    [("near", 2), ("near", 3)]
-    + [("far", 3, g, r) for g in range(3) for r in range(TILES_PER_BLOCK)]
-    + [("pack", 1, r) for r in range(LAST)]
-)
-HALVES = [FIRST, SECOND]
-HELPED_AT = [[3, 6, 8, 10, 12], [3, 5, 7, 9, 11]]
+FIRST = [
+    ("far", 1, 0, 0), ("pack", 0, 0), ("far", 1, 0, 1), ("far", 1, 0, 2), ("pack", 0, 1), ("near", 0), ("near", 1),
+    ("pack", 0, 2), ("far", 2, 0, 1), ("far", 2, 0, 3), ("far", 2, 1, 1), ("far", 2, 1, 3),
+    ("far", 1, 0, 3), ("far", 2, 0, 0), ("far", 2, 0, 2), ("far", 2, 1, 0), ("far", 2, 1, 2),
+]
+SECOND = [
+    ("far", 3, 0, 0), ("pack", 1, 0), ("far", 3, 0, 2), ("far", 3, 1, 0), ("pack", 1, 1), ("near", 2), ("near", 3),
+    ("pack", 1, 2), ("far", 3, 1, 2), ("far", 3, 2, 0), ("far", 3, 2, 2), ("far", 3, 2, 3),
+    ("far", 3, 0, 1), ("far", 3, 0, 3), ("far", 3, 1, 1), ("far", 3, 1, 3), ("far", 3, 2, 1),
+]
+CLOSING = [
+    ("far", 3, 2, 1), ("pack", 1, 0), ("near", 2), ("far", 3, 0, 2), ("pack", 1, 1), ("far", 3, 1, 2), ("far", 3, 2, 2),
+    ("pack", 1, 2), ("far", 3, 0, 3), ("far", 3, 1, 3), ("far", 3, 2, 3), ("near", 3),
+    ("far", 3, 0, 0), ("far", 3, 1, 0), ("far", 3, 2, 0), ("far", 3, 0, 1), ("far", 3, 1, 1),
+]
+HELPED = {
+    "opening": [("far", 1, 0, 3), ("far", 2, 0, 0), ("far", 2, 0, 2), ("far", 2, 1, 0), ("far", 2, 1, 2)],
+    "first": FIRST[DIRECT:],
+    "second": SECOND[DIRECT:],
+    "closing": CLOSING[DIRECT:],
+}
 
 
 def widths(n):
@@ -76,23 +105,30 @@ def tile_tnlattention_pa_kernel(tc, q, k, v, log_slope, out):
 
         rows_of = {}
 
-        def load(h, split):
+        def load(h, pieces):
             k_rows = rows.tile([P, N_BLOCKS, PACK, HEAD_DIM], BF16)
             q_rows = rows.tile([P, N_BLOCKS, TILES_PER_BLOCK, HEAD_DIM], BF16)
             v_rows = rows.tile([P, N_BLOCKS, PACK, HEAD_DIM], BF16)
             k_src = k[0, h].rearrange("(g p t) d -> p g t d", p=P, t=PACK)
             v_src = v[0, h].rearrange("(g p t) d -> p g t d", p=P, t=PACK)
             q_src = q[0, h].rearrange("(b r p) d -> p b r d", p=P, r=TILES_PER_BLOCK)
-            for lo, hi in split:
-                nc.sync.dma_start(out=k_rows[:, lo:hi], in_=k_src[:, lo:hi])
-                nc.sync.dma_start(out=q_rows[:, lo:hi], in_=q_src[:, lo:hi])
-            nc.sync.dma_start(out=v_rows[:], in_=v_src)
+            for which, lo, hi in pieces:
+                rows_tile, src = {"k": (k_rows, k_src), "q": (q_rows, q_src), "v": (v_rows, v_src)}[which]
+                nc.sync.dma_start(out=rows_tile[:, lo:hi], in_=src[:, lo:hi])
             rows_of[h] = (k_rows, q_rows, v_rows)
 
-        slope_bf = const.tile([P, HEADS], BF16)
-        nc.sync.dma_start(out=slope_bf[:], in_=log_slope.partition_broadcast(P))
-        load(0, [(0, 1), (1, 2), (2, N_BLOCKS)])
-        load(1, [(0, N_BLOCKS)])
+        whole = [("k", 0, N_BLOCKS), ("q", 0, N_BLOCKS), ("v", 0, N_BLOCKS)]
+        slope_row = const.tile([P, HEADS], BF16)
+        nc.vector.memset(slope_row[:], 0.0)
+        nc.sync.dma_start(out=slope_row[0:1], in_=log_slope.rearrange("(a h) -> a h", a=1))
+        load(0, [("k", 0, 1), ("q", 1, 2), ("k", 1, 2), ("q", 0, 1), ("q", 2, 4), ("k", 2, 4), ("v", 0, 4)])
+        load(1, whole)
+        warm = const.tile([P, 1], F32)
+        nc.vector.memset(warm[:], 0.0)
+        warmed = const.tile([P, 1], F32)
+        nc.scalar.activation(out=warmed[:], in_=warm[:], func=ACT.Exp)
+        ones = const.tile([P, P], BF16)
+        nc.vector.memset(ones[:], 1.0)
 
         ident = const.tile([P, P], BF16)
         make_identity(nc, ident[:])
@@ -128,28 +164,20 @@ def tile_tnlattention_pa_kernel(tc, q, k, v, log_slope, out):
 
         zero_set(0)
 
+        l_bank = psum_l.tile([P, HEADS], F32)
+        nc.tensor.matmul(l_bank[:], lhsT=ones[:], rhs=slope_row[:], start=True, stop=True)
         slope = const.tile([P, HEADS], F32)
-        nc.vector.tensor_scalar_min(out=slope[:], in0=slope_bf[:], scalar1=-TINY)
+        nc.vector.tensor_scalar_min(out=slope[:], in0=l_bank[:], scalar1=-TINY)
         slope_tile = const.tile([P, HEADS], F32)
         nc.vector.tensor_scalar_mul(out=slope_tile[:], in0=slope[:], scalar1=float(P))
         dist = const.tile([P, P, PACK], F32)
         nc.vector.tensor_copy(out=dist[:], in_=dist_int[:])
         step = const.tile([P, FAR_STEPS], F32)
         nc.vector.tensor_copy(out=step[:], in_=step_int[:])
-        causal = const.tile([P, 1 + LAST, P, PACK], F32)
+        causal = const.tile([P, P, PACK], F32)
         nc.vector.scalar_tensor_tensor(
-            out=causal[:, LAST], in0=dist[:], scalar=-FOREVER, in1=dist[:], op0=ALU.mult, op1=ALU.max
+            out=causal[:], in0=dist[:], scalar=-FOREVER, in1=dist[:], op0=ALU.mult, op1=ALU.max
         )
-        shift = const.tile([P, LAST], F32)
-        nc.vector.memset(shift[:], 0.0)
-        for r in range(LAST):
-            nc.vector.memset(shift[0 : (LAST - r) * STEP, r : r + 1], -float(P * (1 + r)))
-            moved = const.tile([P, P, PACK], F32)
-            nc.vector.tensor_scalar_add(out=moved[:], in0=dist[:], scalar1=shift[:, r : r + 1])
-            nc.vector.scalar_tensor_tensor(
-                out=causal[:, r], in0=moved[:], scalar=-FOREVER, in1=moved[:], op0=ALU.mult, op1=ALU.max
-            )
-
         q_cols_of = {}
         k_odd_of = {}
         table_of = {}
@@ -157,48 +185,64 @@ def tile_tnlattention_pa_kernel(tc, q, k, v, log_slope, out):
         v_grouped_of = {}
         v_codes_of = {}
 
-        def flip(tiles):
-            flipped = psum_t.tile([P, PACK, P], BF16)
+        def flip(tiles, dst, early):
+            if early == 1:
+                s_bank = psum_s.tile([P, PACK, P], BF16)
+                flipped = s_bank
+            elif early == 2:
+                o_bank = psum_o.tile([P, PACK, P], BF16)
+                flipped = o_bank
+            else:
+                t_bank = psum_t.tile([P, PACK, P], BF16)
+                flipped = t_bank
             for j in range(PACK):
                 nc.tensor.transpose(flipped[:, j, :], tiles[:, j, :], ident[:])
-            return flipped
+            if early == 1:
+                nc.vector.tensor_copy(out=dst, in_=flipped[:])
+            else:
+                nc.scalar.copy(out=dst, in_=flipped[:])
 
-        def flip_q(h, b):
+        def flip_q(h, b, early=0):
             if h not in q_cols_of:
                 q_cols = head.tile([P, N_BLOCKS, TILES_PER_BLOCK, P], BF16)
                 q_cols_of[h] = q_cols
-            nc.scalar.copy(out=q_cols_of[h][:, b], in_=flip(rows_of[h][1][:, b])[:])
+            flip(rows_of[h][1][:, b], q_cols_of[h][:, b], early)
 
-        def flip_k(h, g):
+        def flip_k(h, g, early=0):
             if h not in k_odd_of:
                 k_odd = head.tile([P, N_PAIRS, PACK, P], BF16, align_bytes=64)
                 k_odd_of[h] = k_odd
-            flipped = flip(rows_of[h][0][:, g])
             if g % 2 == 0:
-                nc.scalar.copy(out=k_even[h % 2][:, g // 2, :, LAST * STEP :], in_=flipped[:])
+                flip(rows_of[h][0][:, g], k_even[h % 2][:, g // 2, :, LAST * STEP :], early)
             else:
-                nc.scalar.copy(out=k_odd_of[h][:, g // 2], in_=flipped[:])
+                flip(rows_of[h][0][:, g], k_odd_of[h][:, g // 2], early)
                 for r in range(LAST):
                     nc.sync.dma_start(
                         out=k_part[h % 2][:, r, g // 2, :, 0 : (r + 1) * STEP],
                         in_=k_odd_of[h][:, g // 2, :, 0 : (r + 1) * STEP],
                     )
 
-        def decay(h, which):
+        def decay_far(h):
             slope_h = slope[:, h : h + 1]
-            if which == "far":
-                far = head.tile([P, P, PACK], F32)
-                nc.scalar.activation(
-                    out=far[:], in_=dist[:], func=ACT.Exp, bias=slope_tile[:, h : h + 1], scale=slope_h
-                )
-                table_of[(h, "far")] = far
-                far_step = head.tile([P, FAR_STEPS], F32)
-                nc.scalar.activation(out=far_step[:], in_=step[:], func=ACT.Exp, scale=slope_h)
-                far_step_of[h] = far_step
-            else:
-                near = head.tile([P, P, PACK], F32, bufs=2 * (1 + LAST))
-                nc.scalar.activation(out=near[:], in_=causal[:, which], func=ACT.Exp, scale=slope_h)
-                table_of[(h, which)] = near
+            far = head.tile([P, P, PACK], F32)
+            nc.scalar.activation(
+                out=far[:], in_=dist[:], func=ACT.Exp, bias=slope_tile[:, h : h + 1], scale=slope_h
+            )
+            table_of[(h, "far")] = far
+            far_step = head.tile([P, FAR_STEPS], F32)
+            nc.scalar.activation(out=far_step[:], in_=step[:], func=ACT.Exp, scale=slope_h)
+            far_step_of[h] = far_step
+
+        def decay_near(h):
+            near = head.tile([P, P, PACK], F32)
+            nc.scalar.activation(out=near[:], in_=causal[:], func=ACT.Exp, scale=slope[:, h : h + 1])
+            table_of[(h, LAST)] = near
+            for r in range(LAST):
+                pack = head.tile([P, P, PACK], F32, bufs=2 * LAST)
+                low = (LAST - r) * STEP
+                nc.sync.dma_start(out=pack[low:P], in_=near[low:P])
+                nc.sync.dma_start(out=pack[0:low], in_=near[P - low : P])
+                table_of[(h, r)] = pack
 
         def regroup_v(h, g):
             if g == 0:
@@ -238,8 +282,9 @@ def tile_tnlattention_pa_kernel(tc, q, k, v, log_slope, out):
         for c, (h, i) in enumerate(halves):
             helped = []
             direct = 0
-            for at, tile in enumerate(HALVES[i]):
-                if at in HELPED_AT[i]:
+            kind = ("opening" if h == 0 else "first") if i == 0 else "second" if h + 1 < HEADS else "closing"
+            for tile in {"opening": OPENING, "first": FIRST, "second": SECOND, "closing": CLOSING}[kind]:
+                if tile in HELPED[kind]:
                     slot = DIRECT + len(helped)
                     helped.append((slot, h, tile))
                 else:
@@ -337,136 +382,175 @@ def tile_tnlattention_pa_kernel(tc, q, k, v, log_slope, out):
                 out=helped_of[c][:, i], in0=lifted_of[(c, i)][:], in1=table(h, tile)[:], op=ALU.mult
             )
 
-        def quantise(c):
-            e_codes = work.tile([P, CYCLE, P], U32, align_bytes=64, bufs=3)
-            e_scales = work.tile([P, CYCLE, P], U8, align_bytes=64, bufs=3)
-            codes_of[c] = (e_codes, e_scales)
-            for source, base, n in ((energy_of[c], 0, DIRECT), (helped_of[c], DIRECT, HELP)):
-                for at, w in widths(n):
-                    slots = slice(base + at, base + at + w)
-                    nc.vector.quantize_mx(
-                        out=e_codes[:, slots].rearrange("p s c -> p (s c)").bitcast(FP8X4),
-                        scales=e_scales[:, slots].rearrange("p s c -> p (s c)"),
-                        in_=source[:, at : at + w].rearrange("p s c t -> p (s c t)"),
-                    )
-
-        def second_matmul(h, b):
-            o_bank = psum_o.tile([P, TILES_PER_BLOCK, HEAD_DIM], F32)
-            for r in range(TILES_PER_BLOCK):
-                passes = []
-                for g in range(b):
-                    passes.append((("far", b, g, r), v_codes_of[h][:, g], v_scales[h % 2][:, g]))
-                j, odd = b // 2, b % 2
-                if r == LAST:
-                    passes.append((("near", b), v_codes_of[h][:, b], v_scales[h % 2][:, b]))
-                elif odd:
-                    passes.append((("pack", j, LAST - 1 - r), v_part[h % 2][:, 1, r, j], v_scales[h % 2][:, b]))
+        def quantise(c, first, last):
+            if c not in codes_of:
+                e_codes = work.tile([P, CYCLE, P], U32, align_bytes=64, bufs=3)
+                e_scales = work.tile([P, CYCLE, P], U8, align_bytes=64, bufs=3)
+                codes_of[c] = (e_codes, e_scales)
+            e_codes, e_scales = codes_of[c]
+            for at, w in widths(last - first):
+                slots = slice(first + at, first + at + w)
+                if first < DIRECT:
+                    source = energy_of[c][:, slots]
                 else:
-                    passes.append((("pack", j, r), v_part[h % 2][:, 0, r, j], vs_part[h % 2][:, r, j]))
-                for i, (tile, v_words, v_sc) in enumerate(passes):
-                    c, slot = place[(h, tile)]
-                    e_codes, e_scales = codes_of[c]
-                    nc.tensor.matmul_mx(
-                        out=o_bank[:, r, :],
-                        lhsT=e_codes[:, slot].bitcast(FP8X4),
-                        lhsT_scale=e_scales[:, slot],
-                        rhs=v_words.bitcast(FP8X4),
-                        rhs_scale=v_sc,
-                        start=(i == 0),
-                        stop=(i == len(passes) - 1),
-                    )
-            o_rows = work.tile([P, TILES_PER_BLOCK, HEAD_DIM], F32)
-            nc.scalar.copy(out=o_rows[:], in_=o_bank[:])
+                    source = helped_of[c][:, first + at - DIRECT : first + at - DIRECT + w]
+                nc.vector.quantize_mx(
+                    out=e_codes[:, slots].rearrange("p s c -> p (s c)").bitcast(FP8X4),
+                    scales=e_scales[:, slots].rearrange("p s c -> p (s c)"),
+                    in_=source.rearrange("p s c t -> p (s c t)"),
+                )
+
+        o_bank_of = {}
+
+        def second_matmul(h, b, r):
+            if r == 0:
+                o_bank = psum_o.tile([P, TILES_PER_BLOCK, HEAD_DIM], F32)
+                o_bank_of[(h, b)] = o_bank
+            passes = []
+            for g in range(b):
+                passes.append((("far", b, g, r), v_codes_of[h][:, g], v_scales[h % 2][:, g]))
+            j, odd = b // 2, b % 2
+            if r == LAST:
+                passes.append((("near", b), v_codes_of[h][:, b], v_scales[h % 2][:, b]))
+            elif odd:
+                passes.append((("pack", j, LAST - 1 - r), v_part[h % 2][:, 1, r, j], v_scales[h % 2][:, b]))
+            else:
+                passes.append((("pack", j, r), v_part[h % 2][:, 0, r, j], vs_part[h % 2][:, r, j]))
+            for i, (tile, v_words, v_sc) in enumerate(passes):
+                c, slot = place[(h, tile)]
+                e_codes, e_scales = codes_of[c]
+                nc.tensor.matmul_mx(
+                    out=o_bank_of[(h, b)][:, r, :],
+                    lhsT=e_codes[:, slot].bitcast(FP8X4),
+                    lhsT_scale=e_scales[:, slot],
+                    rhs=v_words.bitcast(FP8X4),
+                    rhs_scale=v_sc,
+                    start=(i == 0),
+                    stop=(i == len(passes) - 1),
+                )
+
+        def store(h, b, first, last):
+            if first == 0:
+                o_rows = work.tile([P, TILES_PER_BLOCK, HEAD_DIM], F32)
+                o_rows_of[(h, b)] = o_rows
+            o_rows = o_rows_of[(h, b)]
+            nc.scalar.copy(out=o_rows[:, first:last], in_=o_bank_of[(h, b)][:, first:last])
             nc.sync.dma_start(
-                out=out[0, h, b * BLOCK : (b + 1) * BLOCK, :].rearrange("(r p) d -> p r d", p=P),
-                in_=o_rows[:],
+                out=out[0, h, b * BLOCK + first * P : b * BLOCK + last * P, :].rearrange("(r p) d -> p r d", p=P),
+                in_=o_rows[:, first:last],
             )
+
+        o_rows_of = {}
+
+        def block_step(h, b, r):
+            second_matmul(h, b, r)
+            if r == LAST:
+                store(h, b, 0, TILES_PER_BLOCK)
 
         def chore(c, s):
             h, i = halves[c]
-            nxt = h + 1 if h + 1 < HEADS else None
+            nxt = h + 1
             if i == 0:
                 if s == 0 and h + 2 < HEADS:
-                    load(h + 2, [(0, N_BLOCKS)])
-                if s == 0 and h > 0:
-                    second_matmul(h - 1, 2)
-                if s == 4 and h > 0:
-                    second_matmul(h - 1, 3)
+                    load(h + 2, whole)
+                if h > 0:
+                    if s in A_MX2:
+                        second_matmul(h - 1, 2, A_MX2.index(s))
+                    if s in A_MX3:
+                        second_matmul(h - 1, 3, A_MX3.index(s))
+                    if s == A_O2:
+                        store(h - 1, 2, 0, TILES_PER_BLOCK)
+                    if s == A_O3:
+                        store(h - 1, 3, 0, TILES_PER_BLOCK)
+                if h > 0:
+                    for at, what, which in A_OWN:
+                        if s == at:
+                            what_of[what](h, which)
+                if nxt < HEADS:
+                    for at, what, which in A_PREP:
+                        if s == at:
+                            what_of[what](nxt, which)
             else:
-                if s == 0:
-                    second_matmul(h, 0)
-                if s == 3:
-                    second_matmul(h, 1)
-            if nxt is None:
-                return
-            if i == 0:
-                if s in (1, 3, 5, 7):
-                    flip_k(nxt, s // 2)
-                if s in (9, 11):
-                    flip_q(nxt, (s - 7) // 2)
-                if s == 2:
-                    decay(nxt, "far")
-                if s in (6, 8, 10):
-                    decay(nxt, (LAST, 0, 1)[s // 2 - 3])
-            else:
-                if s in (1, 2, 4, 5):
-                    regroup_v(nxt, (1, 2, 4, 5).index(s))
-                if s == 6:
-                    flip_q(nxt, 0)
-                if s == 8:
-                    flip_q(nxt, 3)
-                if s == 10:
-                    decay(nxt, 2)
+                if s in B_MX0:
+                    for r in range(B_MX0.index(s) * 2, B_MX0.index(s) * 2 + 2):
+                        second_matmul(h, 0, r)
+                if s in B_MX1:
+                    second_matmul(h, 1, B_MX1.index(s))
+                if s == B_O0:
+                    store(h, 0, 0, TILES_PER_BLOCK)
+                if s == B_O1:
+                    store(h, 1, 0, TILES_PER_BLOCK)
+                if nxt < HEADS:
+                    for at, what, which in B_PREP:
+                        if s == at:
+                            what_of[what](nxt, which)
 
-        flip_k(0, 0)
-        flip_q(0, 1)
-        decay(0, "far")
+        what_of = {
+            "k": flip_k,
+            "q": flip_q,
+            "v": regroup_v,
+            "far": lambda h, which: decay_far(h),
+            "near": lambda h, which: decay_near(h),
+        }
+
+        flip_k(0, 0, 1)
+        flip_q(0, 1, 2)
+        decay_far(0)
         fill(0)
         fill(1)
-        lift(0, 0)
-        fill(2)
-        flip_q(0, 0)
         flip_k(0, 1)
-        decay(0, LAST)
+        decay_near(0)
+        flip_q(0, 0, 2)
+        fill(2)
         fill(3)
+        lift(0, 0)
         help_multiply(0, 0)
-        flip_q(0, 2)
-        flip_q(0, 3)
+        flip_q(0, 2, 2)
         n = 0
         for c in range(len(halves)):
+            h, i = halves[c]
+            closing = c + 1 == len(halves)
+            lift_at = LIFT_AT[i] if c > 0 else LIFT_0
             for s in range(DIRECT):
                 multiply(n)
                 if n + BANKS < len(direct_tiles):
                     fill(n + BANKS)
                 if c == 0:
-                    if s in (0, 2, 4, 6):
-                        lift(0, s // 2 + 1)
-                        help_multiply(0, s // 2 + 1)
-                    if s == 1:
-                        flip_k(0, 2)
-                    if s == 3:
-                        flip_k(0, 3)
-                    if s in (5, 6, 7):
-                        decay(0, s - 5)
-                    if s in (7, 8, 9, 10):
-                        regroup_v(0, s - 7)
+                    if s in START_LIFT:
+                        lift(0, 1 + START_LIFT.index(s))
+                        help_multiply(0, 1 + START_LIFT.index(s))
+                    for at, what, which in START_PREP:
+                        if s == at:
+                            what_of[what](0, which)
+                if not closing and s in lift_at:
+                    lift(c + 1, lift_at.index(s))
                 chore(c, s)
+                if closing and s == 9:
+                    quantise(c, 0, 8)
                 n += 1
-            if c + 1 < len(halves):
-                for i in range(HELP):
-                    lift(c + 1, i)
-            h, i = halves[c]
-            if c == 0:
-                quantise_v(0)
-                spread_v(0)
-            if i == 1 and h + 1 < HEADS:
-                quantise_v(h + 1)
-                spread_v(h + 1)
-            quantise(c)
-            if c + 1 < len(halves):
-                for i in range(HELP):
-                    help_multiply(c + 1, i)
+            if closing:
+                break
+            for j in range(len(lift_at), HELP):
+                lift(c + 1, j)
             if c == 0:
                 zero_set(1)
-        second_matmul(HEADS - 1, 2)
-        second_matmul(HEADS - 1, 3)
+            if i == 0 and c > 0:
+                quantise_v(h)
+                spread_v(h)
+            quantise(c, 0, DIRECT)
+            quantise(c, DIRECT, CYCLE)
+            if c == 0:
+                quantise_v(h)
+                spread_v(h)
+            for j in range(HELP):
+                help_multiply(c + 1, j)
+        quantise(c, DIRECT, CYCLE)
+        quantise(c, 8, DIRECT)
+        for r in range(TILES_PER_BLOCK):
+            second_matmul(HEADS - 1, 2, r)
+        store(HEADS - 1, 2, 0, TILES_PER_BLOCK)
+        for r in range(TILES_PER_BLOCK):
+            second_matmul(HEADS - 1, 3, r)
+            if r == LAST - 1:
+                store(HEADS - 1, 3, 0, LAST)
+        store(HEADS - 1, 3, LAST, TILES_PER_BLOCK)

@@ -29,9 +29,11 @@ TINY = 2.0**-60
 
 FLOPS = 2 * 2 * HEADS * HEAD_DIM * BLOCK * BLOCK * (N_BLOCKS * (N_BLOCKS + 1) // 2)
 
-CYCLE = 17
-HELP = 5
-DIRECT = CYCLE - HELP
+PHASES = ((7, 3), (5, 2))
+DIRECT = sum(d for d, e in PHASES)
+HELP = sum(e for d, e in PHASES)
+WIDEST = max(d + e for d, e in PHASES)
+CODE_BUFS = 6
 A_MX2 = (0, 1, 2, 3)
 A_O2 = 4
 A_MX3 = (6, 7, 8, 9)
@@ -276,23 +278,28 @@ def tile_tnlattention_pa_kernel(tc, q, k, v, log_slope, out):
                 )
 
         halves = [(h, i) for h in range(HEADS) for i in range(2)]
+        phases = []
         direct_tiles = []
         helped_tiles = []
         place = {}
-        for c, (h, i) in enumerate(halves):
-            helped = []
-            direct = 0
+        for h, i in halves:
             kind = ("opening" if h == 0 else "first") if i == 0 else "second" if h + 1 < HEADS else "closing"
-            for tile in {"opening": OPENING, "first": FIRST, "second": SECOND, "closing": CLOSING}[kind]:
-                if tile in HELPED[kind]:
-                    slot = DIRECT + len(helped)
-                    helped.append((slot, h, tile))
-                else:
-                    slot = direct
-                    direct_tiles.append((c, slot, h, tile))
-                    direct += 1
-                place[(h, tile)] = (c, slot)
-            helped_tiles.append(helped)
+            tiles = {"opening": OPENING, "first": FIRST, "second": SECOND, "closing": CLOSING}[kind]
+            direct = [tile for tile in tiles if tile not in HELPED[kind]]
+            helped = list(HELPED[kind])
+            for n_direct, n_helped in PHASES:
+                p = len(phases)
+                phases.append((len(direct_tiles), len(helped_tiles), n_direct, n_helped))
+                for j in range(n_direct + n_helped):
+                    if j < n_direct:
+                        tile = direct[j]
+                        direct_tiles.append((p, j, h, tile))
+                    else:
+                        tile = helped[j - n_direct]
+                        helped_tiles.append((p, j - n_direct, h, tile))
+                    place[(h, tile)] = (p, j)
+                direct = direct[n_direct:]
+                helped = helped[n_helped:]
 
         def product(bank, h, tile):
             def k_cols(g, t):
@@ -341,19 +348,19 @@ def tile_tnlattention_pa_kernel(tc, q, k, v, log_slope, out):
         codes_of = {}
 
         def fill(n):
-            c, slot, h, tile = direct_tiles[n]
+            p, slot, h, tile = direct_tiles[n]
             s_bank = psum_s.tile([P, PACK, P], F32)
             product(s_bank, h, tile)
             bank_of[n] = s_bank
 
 
         def multiply(n):
-            c, slot, h, tile = direct_tiles[n]
+            p, slot, h, tile = direct_tiles[n]
             if slot == 0:
-                energy = work.tile([P, DIRECT, P, PACK], BF16, align_bytes=64)
-                energy_of[c] = energy
+                energy = work.tile([P, phases[p][2], P, PACK], BF16, align_bytes=64)
+                energy_of[p] = energy
             s_view = bank_of[n][:].rearrange("p t c -> p c t")
-            dst = energy_of[c][:, slot]
+            dst = energy_of[p][:, slot]
             if tile[0] == "far":
                 nc.vector.scalar_tensor_tensor(
                     out=dst, in0=s_view, scalar=far_scalar(h, tile), in1=table(h, tile)[:], op0=ALU.mult, op1=ALU.mult
@@ -361,8 +368,8 @@ def tile_tnlattention_pa_kernel(tc, q, k, v, log_slope, out):
             else:
                 nc.vector.tensor_tensor(out=dst, in0=s_view, in1=table(h, tile)[:], op=ALU.mult)
 
-        def lift(c, i):
-            slot, h, tile = helped_tiles[c][i]
+        def lift(m):
+            p, at, h, tile = helped_tiles[m]
             l_bank = psum_l.tile([P, PACK, P], F32)
             product(l_bank, h, tile)
             s_view = l_bank[:].rearrange("p t c -> p c t")
@@ -371,34 +378,38 @@ def tile_tnlattention_pa_kernel(tc, q, k, v, log_slope, out):
                 nc.scalar.activation(out=lifted[:], in_=s_view, func=ACT.Copy, scale=far_scalar(h, tile))
             else:
                 nc.scalar.copy(out=lifted[:], in_=s_view)
-            lifted_of[(c, i)] = lifted
+            lifted_of[m] = lifted
 
-        def help_multiply(c, i):
-            slot, h, tile = helped_tiles[c][i]
-            if i == 0:
-                helped = work.tile([P, HELP, P, PACK], BF16, align_bytes=64, bufs=1)
-                helped_of[c] = helped
+        def help_multiply(m):
+            p, at, h, tile = helped_tiles[m]
+            if at == 0:
+                helped = work.tile([P, phases[p][3], P, PACK], BF16, align_bytes=64, bufs=1)
+                helped_of[p] = helped
             nc.gpsimd.tensor_tensor(
-                out=helped_of[c][:, i], in0=lifted_of[(c, i)][:], in1=table(h, tile)[:], op=ALU.mult
+                out=helped_of[p][:, at], in0=lifted_of[m][:], in1=table(h, tile)[:], op=ALU.mult
             )
 
-        def quantise(c, first, last):
-            if c not in codes_of:
-                e_codes = work.tile([P, CYCLE, P], U32, align_bytes=64, bufs=3)
-                e_scales = work.tile([P, CYCLE, P], U8, align_bytes=64, bufs=3)
-                codes_of[c] = (e_codes, e_scales)
-            e_codes, e_scales = codes_of[c]
-            for at, w in widths(last - first):
-                slots = slice(first + at, first + at + w)
-                if first < DIRECT:
-                    source = energy_of[c][:, slots]
-                else:
-                    source = helped_of[c][:, first + at - DIRECT : first + at - DIRECT + w]
+        def help_phase(p):
+            for m in range(phases[p][1], phases[p][1] + phases[p][3]):
+                help_multiply(m)
+
+        def quantise(p, source, base):
+            if p not in codes_of:
+                e_codes = work.tile([P, WIDEST, P], U32, align_bytes=64, bufs=CODE_BUFS)
+                e_scales = work.tile([P, WIDEST, P], U8, align_bytes=64, bufs=CODE_BUFS)
+                codes_of[p] = (e_codes, e_scales)
+            e_codes, e_scales = codes_of[p]
+            for at, w in widths(source.shape[1]):
+                slots = slice(base + at, base + at + w)
                 nc.vector.quantize_mx(
                     out=e_codes[:, slots].rearrange("p s c -> p (s c)").bitcast(FP8X4),
                     scales=e_scales[:, slots].rearrange("p s c -> p (s c)"),
-                    in_=source.rearrange("p s c t -> p (s c t)"),
+                    in_=source[:, at : at + w].rearrange("p s c t -> p (s c t)"),
                 )
+
+        def quantise_phase(p):
+            quantise(p, energy_of[p][:], 0)
+            quantise(p, helped_of[p][:], phases[p][2])
 
         o_bank_of = {}
 
@@ -417,8 +428,8 @@ def tile_tnlattention_pa_kernel(tc, q, k, v, log_slope, out):
             else:
                 passes.append((("pack", j, r), v_part[h % 2][:, 0, r, j], vs_part[h % 2][:, r, j]))
             for i, (tile, v_words, v_sc) in enumerate(passes):
-                c, slot = place[(h, tile)]
-                e_codes, e_scales = codes_of[c]
+                p, slot = place[(h, tile)]
+                e_codes, e_scales = codes_of[p]
                 nc.tensor.matmul_mx(
                     out=o_bank_of[(h, b)][:, r, :],
                     lhsT=e_codes[:, slot].bitcast(FP8X4),
@@ -503,8 +514,8 @@ def tile_tnlattention_pa_kernel(tc, q, k, v, log_slope, out):
         flip_q(0, 0, 2)
         fill(2)
         fill(3)
-        lift(0, 0)
-        help_multiply(0, 0)
+        lift(0)
+        help_multiply(0)
         flip_q(0, 2, 2)
         n = 0
         for c in range(len(halves)):
@@ -517,35 +528,36 @@ def tile_tnlattention_pa_kernel(tc, q, k, v, log_slope, out):
                     fill(n + BANKS)
                 if c == 0:
                     if s in START_LIFT:
-                        lift(0, 1 + START_LIFT.index(s))
-                        help_multiply(0, 1 + START_LIFT.index(s))
+                        lift(1 + START_LIFT.index(s))
+                        if START_LIFT.index(s) + 1 < PHASES[0][1]:
+                            help_multiply(1 + START_LIFT.index(s))
                     for at, what, which in START_PREP:
                         if s == at:
                             what_of[what](0, which)
                 if not closing and s in lift_at:
-                    lift(c + 1, lift_at.index(s))
+                    lift((c + 1) * HELP + lift_at.index(s))
                 chore(c, s)
-                if closing and s == 9:
-                    quantise(c, 0, 8)
                 n += 1
+                if s == PHASES[0][0] - 1:
+                    quantise_phase(2 * c)
+                    help_phase(2 * c + 1)
             if closing:
                 break
             for j in range(len(lift_at), HELP):
-                lift(c + 1, j)
+                lift((c + 1) * HELP + j)
             if c == 0:
                 zero_set(1)
             if i == 0 and c > 0:
                 quantise_v(h)
                 spread_v(h)
-            quantise(c, 0, DIRECT)
-            quantise(c, DIRECT, CYCLE)
+            quantise_phase(2 * c + 1)
             if c == 0:
                 quantise_v(h)
                 spread_v(h)
-            for j in range(HELP):
-                help_multiply(c + 1, j)
-        quantise(c, DIRECT, CYCLE)
-        quantise(c, 8, DIRECT)
+            help_phase(2 * c + 2)
+        last = len(phases) - 1
+        quantise(last, helped_of[last][:], phases[last][2])
+        quantise(last, energy_of[last][:], 0)
         for r in range(TILES_PER_BLOCK):
             second_matmul(HEADS - 1, 2, r)
         store(HEADS - 1, 2, 0, TILES_PER_BLOCK)

@@ -29,10 +29,13 @@ TINY = 2.0**-60
 
 FLOPS = 2 * 2 * HEADS * HEAD_DIM * BLOCK * BLOCK * (N_BLOCKS * (N_BLOCKS + 1) // 2)
 
-PHASES = ((7, 3), (5, 2))
-DIRECT = sum(d for d, e in PHASES)
-HELP = sum(e for d, e in PHASES)
-WIDEST = max(d + e for d, e in PHASES)
+SPLIT = ((8, 4), (4, 1))
+OPEN = ((8, 2), (5, 2))
+PHASES = {"opening": OPEN, "first": SPLIT, "second": SPLIT, "closing": SPLIT}
+DIRECT = 12
+HELP = 5
+LIFT_BUFS = 4
+WIDEST = 17
 CODE_BUFS = 6
 A_MX2 = (0, 1, 2, 3)
 A_O2 = 4
@@ -46,9 +49,15 @@ B_MX1 = (7, 8, 9, 10)
 B_O1 = 11
 B_PREP = ((0, "q", 0), (2, "k", 2), (3, "k", 3), (4, "near", 0), (8, "q", 3), (9, "v", 0), (10, "v", 1))
 LIFT_AT = ((1, 3, 6, 8), (1, 3, 6, 8))
-LIFT_0 = (4, 5, 6, 8)
-START_LIFT = (0, 1, 2, 3)
-START_PREP = ((0, "q", 3), (2, "k", 2), (4, "k", 3), (6, "v", 0), (7, "v", 1), (8, "v", 2), (9, "v", 3))
+LIFT_0 = (5, 7, 9, 11)
+LIFT_1 = (4, 6, 8, 10)
+A_PREP_0 = ((10, "k", 0), (12, "k", 1))
+B_PREP_0 = (
+    (0, "q", 1), (1, "q", 2), (2, "far", 0), (3, "q", 0), (5, "k", 2), (6, "k", 3), (7, "near", 0), (9, "q", 3),
+    (10, "v", 0), (11, "v", 1),
+)
+START_LIFT = (0, 2, 3)
+START_PREP = ((1, "q", 3), (3, "k", 2), (4, "k", 3), (5, "v", 0), (7, "v", 1), (9, "v", 2), (11, "v", 3))
 BANKS = 4
 
 OPENING = (
@@ -68,12 +77,12 @@ SECOND = [
     ("far", 3, 0, 1), ("far", 3, 0, 3), ("far", 3, 1, 1), ("far", 3, 1, 3), ("far", 3, 2, 1),
 ]
 CLOSING = [
-    ("far", 3, 2, 1), ("pack", 1, 0), ("near", 2), ("far", 3, 0, 2), ("pack", 1, 1), ("far", 3, 1, 2), ("far", 3, 2, 2),
-    ("pack", 1, 2), ("far", 3, 0, 3), ("far", 3, 1, 3), ("far", 3, 2, 3), ("near", 3),
-    ("far", 3, 0, 0), ("far", 3, 1, 0), ("far", 3, 2, 0), ("far", 3, 0, 1), ("far", 3, 1, 1),
+    ("pack", 1, 0), ("far", 3, 0, 1), ("pack", 1, 1), ("far", 3, 1, 1), ("pack", 1, 2), ("far", 3, 2, 1), ("near", 2),
+    ("far", 3, 0, 2), ("far", 3, 0, 3), ("far", 3, 1, 3), ("far", 3, 2, 3), ("near", 3),
+    ("far", 3, 0, 0), ("far", 3, 1, 0), ("far", 3, 2, 0), ("far", 3, 1, 2), ("far", 3, 2, 2),
 ]
 HELPED = {
-    "opening": [("far", 1, 0, 3), ("far", 2, 0, 0), ("far", 2, 0, 2), ("far", 2, 1, 0), ("far", 2, 1, 2)],
+    "opening": [("far", 1, 0, 3), ("far", 2, 0, 0), ("far", 2, 0, 2), ("far", 2, 1, 0)],
     "first": FIRST[DIRECT:],
     "second": SECOND[DIRECT:],
     "closing": CLOSING[DIRECT:],
@@ -282,13 +291,18 @@ def tile_tnlattention_pa_kernel(tc, q, k, v, log_slope, out):
         direct_tiles = []
         helped_tiles = []
         place = {}
+        ends_of = []
         for h, i in halves:
             kind = ("opening" if h == 0 else "first") if i == 0 else "second" if h + 1 < HEADS else "closing"
             tiles = {"opening": OPENING, "first": FIRST, "second": SECOND, "closing": CLOSING}[kind]
             direct = [tile for tile in tiles if tile not in HELPED[kind]]
             helped = list(HELPED[kind])
-            for n_direct, n_helped in PHASES:
+            phase_ends = []
+            done = 0
+            for n_direct, n_helped in PHASES[kind]:
                 p = len(phases)
+                done += n_direct
+                phase_ends.append((done, p))
                 phases.append((len(direct_tiles), len(helped_tiles), n_direct, n_helped))
                 for j in range(n_direct + n_helped):
                     if j < n_direct:
@@ -300,6 +314,7 @@ def tile_tnlattention_pa_kernel(tc, q, k, v, log_slope, out):
                     place[(h, tile)] = (p, j)
                 direct = direct[n_direct:]
                 helped = helped[n_helped:]
+            ends_of.append(phase_ends)
 
         def product(bank, h, tile):
             def k_cols(g, t):
@@ -370,28 +385,29 @@ def tile_tnlattention_pa_kernel(tc, q, k, v, log_slope, out):
 
         def lift(m):
             p, at, h, tile = helped_tiles[m]
+            if at == 0:
+                lifted = work.tile([P, phases[p][3], P, PACK], F32, bufs=LIFT_BUFS)
+                lifted_of[p] = lifted
             l_bank = psum_l.tile([P, PACK, P], F32)
             product(l_bank, h, tile)
-            s_view = l_bank[:].rearrange("p t c -> p c t")
-            lifted = work.tile([P, P, PACK], F32, bufs=2 * HELP)
-            if tile[0] == "far":
-                nc.scalar.activation(out=lifted[:], in_=s_view, func=ACT.Copy, scale=far_scalar(h, tile))
-            else:
-                nc.scalar.copy(out=lifted[:], in_=s_view)
-            lifted_of[m] = lifted
-
-        def help_multiply(m):
-            p, at, h, tile = helped_tiles[m]
-            if at == 0:
-                helped = work.tile([P, phases[p][3], P, PACK], BF16, align_bytes=64, bufs=1)
-                helped_of[p] = helped
-            nc.gpsimd.tensor_tensor(
-                out=helped_of[p][:, at], in0=lifted_of[m][:], in1=table(h, tile)[:], op=ALU.mult
+            nc.scalar.activation(
+                out=lifted_of[p][:, at],
+                in_=l_bank[:].rearrange("p t c -> p c t"),
+                func=ACT.Copy,
+                scale=far_scalar(h, tile),
             )
 
         def help_phase(p):
-            for m in range(phases[p][1], phases[p][1] + phases[p][3]):
-                help_multiply(m)
+            m, n_helped = phases[p][1], phases[p][3]
+            h = helped_tiles[m][2]
+            helped = work.tile([P, n_helped, P * PACK], BF16, align_bytes=64, bufs=1)
+            nc.gpsimd.tensor_tensor(
+                out=helped[:],
+                in0=lifted_of[p][:].rearrange("p s c t -> p s (c t)"),
+                in1=table_of[(h, "far")][:].rearrange("p c t -> p (c t)").unsqueeze(1).to_broadcast([P, n_helped, P * PACK]),
+                op=ALU.mult,
+            )
+            helped_of[p] = helped
 
         def quantise(p, source, base):
             if p not in codes_of:
@@ -404,17 +420,23 @@ def tile_tnlattention_pa_kernel(tc, q, k, v, log_slope, out):
                 nc.vector.quantize_mx(
                     out=e_codes[:, slots].rearrange("p s c -> p (s c)").bitcast(FP8X4),
                     scales=e_scales[:, slots].rearrange("p s c -> p (s c)"),
-                    in_=source[:, at : at + w].rearrange("p s c t -> p (s c t)"),
+                    in_=source[:, at : at + w].rearrange("p s e -> p (s e)"),
                 )
 
         def quantise_phase(p):
-            quantise(p, energy_of[p][:], 0)
+            quantise(p, energy_of[p][:].rearrange("p s c t -> p s (c t)"), 0)
             quantise(p, helped_of[p][:], phases[p][2])
 
         o_bank_of = {}
 
         def second_matmul(h, b, r):
-            if r == 0:
+            if h == HEADS - 1 and b == N_BLOCKS - 1:
+                s_bank = psum_s.tile([P, TILES_PER_BLOCK, HEAD_DIM], F32)
+                o_bank_of[(h, b)] = s_bank
+            elif h == HEADS - 1 and b == N_BLOCKS - 2 and r == 0:
+                l_bank = psum_l.tile([P, TILES_PER_BLOCK, HEAD_DIM], F32)
+                o_bank_of[(h, b)] = l_bank
+            elif (h, b) not in o_bank_of:
                 o_bank = psum_o.tile([P, TILES_PER_BLOCK, HEAD_DIM], F32)
                 o_bank_of[(h, b)] = o_bank
             passes = []
@@ -440,12 +462,16 @@ def tile_tnlattention_pa_kernel(tc, q, k, v, log_slope, out):
                     stop=(i == len(passes) - 1),
                 )
 
-        def store(h, b, first, last):
+        def store(h, b, first, last, by_vector=False):
             if first == 0:
-                o_rows = work.tile([P, TILES_PER_BLOCK, HEAD_DIM], F32)
+                o_rows = work.tile([P, TILES_PER_BLOCK, HEAD_DIM], F32, bufs=3)
                 o_rows_of[(h, b)] = o_rows
             o_rows = o_rows_of[(h, b)]
-            nc.scalar.copy(out=o_rows[:, first:last], in_=o_bank_of[(h, b)][:, first:last])
+            src = o_bank_of[(h, b)][:, first:last]
+            if by_vector:
+                nc.vector.tensor_copy(out=o_rows[:, first:last], in_=src)
+            else:
+                nc.scalar.copy(out=o_rows[:, first:last], in_=src)
             nc.sync.dma_start(
                 out=out[0, h, b * BLOCK + first * P : b * BLOCK + last * P, :].rearrange("(r p) d -> p r d", p=P),
                 in_=o_rows[:, first:last],
@@ -462,7 +488,7 @@ def tile_tnlattention_pa_kernel(tc, q, k, v, log_slope, out):
             h, i = halves[c]
             nxt = h + 1
             if i == 0:
-                if s == 0 and h + 2 < HEADS:
+                if s == (4 if h > 0 else 12) and h + 2 < HEADS:
                     load(h + 2, whole)
                 if h > 0:
                     if s in A_MX2:
@@ -478,7 +504,7 @@ def tile_tnlattention_pa_kernel(tc, q, k, v, log_slope, out):
                         if s == at:
                             what_of[what](h, which)
                 if nxt < HEADS:
-                    for at, what, which in A_PREP:
+                    for at, what, which in A_PREP if h > 0 else A_PREP_0:
                         if s == at:
                             what_of[what](nxt, which)
             else:
@@ -492,7 +518,7 @@ def tile_tnlattention_pa_kernel(tc, q, k, v, log_slope, out):
                 if s == B_O1:
                     store(h, 1, 0, TILES_PER_BLOCK)
                 if nxt < HEADS:
-                    for at, what, which in B_PREP:
+                    for at, what, which in B_PREP if h > 0 else B_PREP_0:
                         if s == at:
                             what_of[what](nxt, which)
 
@@ -515,54 +541,58 @@ def tile_tnlattention_pa_kernel(tc, q, k, v, log_slope, out):
         fill(2)
         fill(3)
         lift(0)
-        help_multiply(0)
         flip_q(0, 2, 2)
         n = 0
+        turn = None
         for c in range(len(halves)):
             h, i = halves[c]
             closing = c + 1 == len(halves)
-            lift_at = LIFT_AT[i] if c > 0 else LIFT_0
-            for s in range(DIRECT):
+            lift_at = LIFT_AT[i] if h > 0 else (LIFT_0, LIFT_1)[i]
+            n_steps = ends_of[c][-1][0]
+            first_lift = phases[ends_of[c][-1][1]][1] + phases[ends_of[c][-1][1]][3]
+            for s in range(n_steps):
                 multiply(n)
+                if turn is not None:
+                    if turn[1] is not None:
+                        quantise_v(turn[1])
+                        spread_v(turn[1])
+                    quantise_phase(turn[0])
+                    help_phase(turn[0] + 1)
+                    turn = None
                 if n + BANKS < len(direct_tiles):
                     fill(n + BANKS)
                 if c == 0:
                     if s in START_LIFT:
-                        lift(1 + START_LIFT.index(s))
-                        if START_LIFT.index(s) + 1 < PHASES[0][1]:
-                            help_multiply(1 + START_LIFT.index(s))
+                        m = 1 + START_LIFT.index(s)
+                        lift(m)
+                        if m + 1 == PHASES["opening"][0][1]:
+                            help_phase(0)
                     for at, what, which in START_PREP:
                         if s == at:
                             what_of[what](0, which)
                 if not closing and s in lift_at:
-                    lift((c + 1) * HELP + lift_at.index(s))
+                    lift(first_lift + lift_at.index(s))
                 chore(c, s)
+                if closing and s >= n_steps - TILES_PER_BLOCK:
+                    second_matmul(HEADS - 1, 2, s - n_steps + TILES_PER_BLOCK)
+                    if s == n_steps - 1:
+                        store(HEADS - 1, 2, 0, TILES_PER_BLOCK)
                 n += 1
-                if s == PHASES[0][0] - 1:
-                    quantise_phase(2 * c)
-                    help_phase(2 * c + 1)
+                for end, p in ends_of[c]:
+                    if s + 1 == end:
+                        turn = (p, h if end == n_steps and i == 0 else None)
             if closing:
+                for r in range(2):
+                    second_matmul(HEADS - 1, 3, r)
+                    store(HEADS - 1, 3, r, r + 1)
                 break
             for j in range(len(lift_at), HELP):
-                lift((c + 1) * HELP + j)
+                lift(first_lift + j)
             if c == 0:
                 zero_set(1)
-            if i == 0 and c > 0:
-                quantise_v(h)
-                spread_v(h)
-            quantise_phase(2 * c + 1)
-            if c == 0:
-                quantise_v(h)
-                spread_v(h)
-            help_phase(2 * c + 2)
         last = len(phases) - 1
         quantise(last, helped_of[last][:], phases[last][2])
-        quantise(last, energy_of[last][:], 0)
-        for r in range(TILES_PER_BLOCK):
-            second_matmul(HEADS - 1, 2, r)
-        store(HEADS - 1, 2, 0, TILES_PER_BLOCK)
-        for r in range(TILES_PER_BLOCK):
+        quantise(last, energy_of[last][:].rearrange("p s c t -> p s (c t)"), 0)
+        for r in (2, LAST):
             second_matmul(HEADS - 1, 3, r)
-            if r == LAST - 1:
-                store(HEADS - 1, 3, 0, LAST)
-        store(HEADS - 1, 3, LAST, TILES_PER_BLOCK)
+            store(HEADS - 1, 3, r, r + 1, by_vector=(r == LAST))

@@ -37,27 +37,26 @@ HELP = 5
 LIFT_BUFS = 4
 WIDEST = 17
 CODE_BUFS = 6
-A_MX2 = (0, 1, 2, 3)
+A_MX2 = (1, 2, 3, 4)
 A_O2 = 4
-A_MX3 = (6, 7, 8, 9)
+A_MX3 = (7, 9, 10, 11)
 A_O3 = 11
-A_OWN = ((0, "v", 2), (2, "v", 3))
-A_PREP = ((3, "k", 0), (5, "k", 1), (7, "q", 1), (8, "q", 2), (9, "far", 0))
-B_MX0 = (4, 5)
-B_O0 = 6
-B_MX1 = (7, 8, 9, 10)
-B_O1 = 11
-B_PREP = ((0, "q", 0), (2, "k", 2), (3, "k", 3), (4, "near", 0), (8, "q", 3), (9, "v", 0), (10, "v", 1))
+A_OWN = ((1, "v", 2), (2, "v", 3))
+A_PREP = ((0, "k", (0, 1)), (8, "q", (0, 1)), (9, "far", 0))
+A_PREP_0 = ((11, "k", (0, 1)),)
+B_MX0 = (1, 1, 2, 2)
+B_MX1 = (5, 6, 7, 9)
+B_MX0_0 = (6, 6, 7, 7)
+B_MX1_0 = (10, 10, 11, 11)
+B_PREP = ((0, "q", (2, 3)), (4, "near", 0), (8, "k", (2, 3)), (9, "v", 0), (10, "v", 1))
+B_PREP_0 = (
+    (0, "q", (0, 1)), (1, "far", 0), (3, "q", (2, 3)), (5, "near", 0), (8, "k", (2, 3)), (10, "v", 0), (11, "v", 1),
+)
 LIFT_AT = ((1, 3, 6, 8), (1, 3, 6, 8))
 LIFT_0 = (5, 7, 9, 11)
 LIFT_1 = (4, 6, 8, 10)
-A_PREP_0 = ((10, "k", 0), (12, "k", 1))
-B_PREP_0 = (
-    (0, "q", 1), (1, "q", 2), (2, "far", 0), (3, "q", 0), (5, "k", 2), (6, "k", 3), (7, "near", 0), (9, "q", 3),
-    (10, "v", 0), (11, "v", 1),
-)
 START_LIFT = (0, 2, 3)
-START_PREP = ((1, "q", 3), (3, "k", 2), (4, "k", 3), (5, "v", 0), (7, "v", 1), (9, "v", 2), (11, "v", 3))
+START_PREP = ((3, "k", (2, 3)), (5, "v", 0), (7, "v", 1), (9, "v", 2), (11, "v", 3))
 BANKS = 4
 
 OPENING = (
@@ -196,42 +195,51 @@ def tile_tnlattention_pa_kernel(tc, q, k, v, log_slope, out):
         v_grouped_of = {}
         v_codes_of = {}
 
-        def flip(tiles, dst, early):
+        def flip(row_tiles, early=0):
+            n_tiles = PACK * len(row_tiles)
             if early == 1:
-                s_bank = psum_s.tile([P, PACK, P], BF16)
+                s_bank = psum_s.tile([P, n_tiles, P], BF16)
                 flipped = s_bank
             elif early == 2:
-                o_bank = psum_o.tile([P, PACK, P], BF16)
+                o_bank = psum_o.tile([P, n_tiles, P], BF16)
                 flipped = o_bank
             else:
-                t_bank = psum_t.tile([P, PACK, P], BF16)
+                t_bank = psum_t.tile([P, n_tiles, P], BF16)
                 flipped = t_bank
-            for j in range(PACK):
-                nc.tensor.transpose(flipped[:, j, :], tiles[:, j, :], ident[:])
-            if early == 1:
-                nc.vector.tensor_copy(out=dst, in_=flipped[:])
-            else:
-                nc.scalar.copy(out=dst, in_=flipped[:])
+            for i, tiles in enumerate(row_tiles):
+                for j in range(PACK):
+                    nc.tensor.transpose(flipped[:, i * PACK + j, :], tiles[:, j, :], ident[:])
+            return flipped
 
-        def flip_q(h, b, early=0):
+        def flip_q(h, blocks, early=0):
             if h not in q_cols_of:
-                q_cols = head.tile([P, N_BLOCKS, TILES_PER_BLOCK, P], BF16)
+                q_cols = head.tile([P, N_BLOCKS * TILES_PER_BLOCK, P], BF16)
                 q_cols_of[h] = q_cols
-            flip(rows_of[h][1][:, b], q_cols_of[h][:, b], early)
+            flipped = flip([rows_of[h][1][:, b] for b in blocks], early)
+            first = blocks[0] * TILES_PER_BLOCK
+            nc.scalar.copy(out=q_cols_of[h][:, first : first + TILES_PER_BLOCK * len(blocks)], in_=flipped[:])
 
-        def flip_k(h, g, early=0):
+        def flip_k(h, groups, early=0):
             if h not in k_odd_of:
                 k_odd = head.tile([P, N_PAIRS, PACK, P], BF16, align_bytes=64)
                 k_odd_of[h] = k_odd
-            if g % 2 == 0:
-                flip(rows_of[h][0][:, g], k_even[h % 2][:, g // 2, :, LAST * STEP :], early)
-            else:
-                flip(rows_of[h][0][:, g], k_odd_of[h][:, g // 2], early)
-                for r in range(LAST):
-                    nc.sync.dma_start(
-                        out=k_part[h % 2][:, r, g // 2, :, 0 : (r + 1) * STEP],
-                        in_=k_odd_of[h][:, g // 2, :, 0 : (r + 1) * STEP],
-                    )
+            flipped = flip([rows_of[h][0][:, g] for g in groups], early)
+            for i, g in enumerate(groups):
+                src = flipped[:, i * PACK : (i + 1) * PACK, :]
+                if g % 2 == 0:
+                    dst = k_even[h % 2][:, g // 2, :, LAST * STEP :]
+                else:
+                    dst = k_odd_of[h][:, g // 2]
+                if early == 1:
+                    nc.vector.tensor_copy(out=dst, in_=src)
+                else:
+                    nc.scalar.copy(out=dst, in_=src)
+                if g % 2 == 1:
+                    for r in range(LAST):
+                        nc.sync.dma_start(
+                            out=k_part[h % 2][:, r, g // 2, :, 0 : (r + 1) * STEP],
+                            in_=k_odd_of[h][:, g // 2, :, 0 : (r + 1) * STEP],
+                        )
 
         def decay_far(h):
             slope_h = slope[:, h : h + 1]
@@ -329,14 +337,14 @@ def tile_tnlattention_pa_kernel(tc, q, k, v, log_slope, out):
                     nc.tensor.matmul(
                         bank[:, t, :],
                         lhsT=k_even[h % 2][:, j, t, r * STEP : r * STEP + P],
-                        rhs=q_cols[:, 2 * j, r],
+                        rhs=q_cols[:, 2 * j * TILES_PER_BLOCK + r],
                         start=True,
                         stop=False,
                     )
                     nc.tensor.matmul(
                         bank[:, t, :],
                         lhsT=k_part[h % 2][:, LAST - 1 - r, j, t],
-                        rhs=q_cols[:, 2 * j + 1, LAST - 1 - r],
+                        rhs=q_cols[:, (2 * j + 1) * TILES_PER_BLOCK + LAST - 1 - r],
                         start=False,
                         stop=True,
                     )
@@ -344,7 +352,7 @@ def tile_tnlattention_pa_kernel(tc, q, k, v, log_slope, out):
                 b = tile[1]
                 g, r = (b, LAST) if tile[0] == "near" else tile[2:]
                 for t in range(PACK):
-                    nc.tensor.matmul(bank[:, t, :], lhsT=k_cols(g, t), rhs=q_cols[:, b, r], start=True, stop=True)
+                    nc.tensor.matmul(bank[:, t, :], lhsT=k_cols(g, t), rhs=q_cols[:, b * TILES_PER_BLOCK + r], start=True, stop=True)
 
         def far_scalar(h, tile):
             kind, b, g, r = tile
@@ -508,15 +516,12 @@ def tile_tnlattention_pa_kernel(tc, q, k, v, log_slope, out):
                         if s == at:
                             what_of[what](nxt, which)
             else:
-                if s in B_MX0:
-                    for r in range(B_MX0.index(s) * 2, B_MX0.index(s) * 2 + 2):
-                        second_matmul(h, 0, r)
-                if s in B_MX1:
-                    second_matmul(h, 1, B_MX1.index(s))
-                if s == B_O0:
-                    store(h, 0, 0, TILES_PER_BLOCK)
-                if s == B_O1:
-                    store(h, 1, 0, TILES_PER_BLOCK)
+                for b, at in enumerate((B_MX0, B_MX1) if h > 0 else (B_MX0_0, B_MX1_0)):
+                    for r in range(TILES_PER_BLOCK):
+                        if s == at[r]:
+                            second_matmul(h, b, r)
+                    if s == at[LAST]:
+                        store(h, b, 0, TILES_PER_BLOCK)
                 if nxt < HEADS:
                     for at, what, which in B_PREP if h > 0 else B_PREP_0:
                         if s == at:
@@ -530,18 +535,18 @@ def tile_tnlattention_pa_kernel(tc, q, k, v, log_slope, out):
             "near": lambda h, which: decay_near(h),
         }
 
-        flip_k(0, 0, 1)
-        flip_q(0, 1, 2)
+        flip_k(0, (0,), 1)
+        flip_q(0, (1,), 2)
         decay_far(0)
         fill(0)
         fill(1)
-        flip_k(0, 1)
+        flip_k(0, (1,))
         decay_near(0)
-        flip_q(0, 0, 2)
+        flip_q(0, (0,), 2)
         fill(2)
         fill(3)
         lift(0)
-        flip_q(0, 2, 2)
+        flip_q(0, (2, 3), 2)
         n = 0
         turn = None
         for c in range(len(halves)):
@@ -580,7 +585,7 @@ def tile_tnlattention_pa_kernel(tc, q, k, v, log_slope, out):
                 n += 1
                 for end, p in ends_of[c]:
                     if s + 1 == end:
-                        turn = (p, h if end == n_steps and i == 0 else None)
+                        turn = (p, h if i == 0 and (end == n_steps) == (h == 0) else None)
             if closing:
                 for r in range(2):
                     second_matmul(HEADS - 1, 3, r)

@@ -41,20 +41,20 @@ A_MX2 = (1, 2, 3, 4)
 A_O2 = 4
 A_MX3 = (7, 9, 10, 11)
 A_O3 = 11
-A_OWN = ((1, "v", 2), (2, "v", 3))
-A_PREP = ((0, "k", (0, 1)), (8, "q", (0, 1)), (9, "far", 0))
+A_PREP = ((0, "k", (0, 1)), (2, "v", 0), (5, "v", 1), (8, "q", (0, 1)), (9, "far", 0))
 A_PREP_0 = ((11, "k", (0, 1)),)
 B_MX0 = (1, 1, 2, 2)
 B_MX1 = (5, 6, 7, 9)
-B_MX0_0 = (6, 6, 7, 7)
-B_MX1_0 = (10, 10, 11, 11)
-B_PREP = ((0, "q", (2, 3)), (4, "near", 0), (8, "k", (2, 3)), (9, "v", 0), (10, "v", 1))
+B_MX0_0 = (9, 9, 9, 9)
+B_MX1_0 = (11, 11, 11, 11)
+B_PREP = ((0, "q", (2, 3)), (1, "v", 2), (3, "v", 3), (4, "near", 0), (8, "k", (2, 3)))
 B_PREP_0 = (
-    (0, "q", (0, 1)), (1, "far", 0), (3, "q", (2, 3)), (5, "near", 0), (8, "k", (2, 3)), (10, "v", 0), (11, "v", 1),
+    (0, "q", (0, 1)), (1, "far", 0), (2, "v", 0), (3, "q", (2, 3)), (4, "v", 1), (5, "near", 0), (6, "v", 2),
+    (8, "k", (2, 3)), (9, "v", 3),
 )
 LIFT_AT = ((1, 3, 6, 8), (1, 3, 6, 8))
 LIFT_0 = (5, 7, 9, 11)
-LIFT_1 = (4, 6, 8, 10)
+LIFT_1 = (4, 7, 8, 10)
 START_LIFT = (0, 2, 3)
 START_PREP = ((3, "k", (2, 3)), (5, "v", 0), (7, "v", 1), (9, "v", 2), (11, "v", 3))
 BANKS = 4
@@ -98,6 +98,10 @@ def widths(n):
         runs.append((at, w))
         at += w
     return runs
+
+
+def pieces(n):
+    return ([(0, 64)] if n >= 64 else []) + ([(n // 64 * 64, 32)] if n % 64 else [])
 
 
 def tile_tnlattention_pa_kernel(tc, q, k, v, log_slope, out):
@@ -259,8 +263,10 @@ def tile_tnlattention_pa_kernel(tc, q, k, v, log_slope, out):
             for r in range(LAST):
                 pack = head.tile([P, P, PACK], F32, bufs=2 * LAST)
                 low = (LAST - r) * STEP
-                nc.sync.dma_start(out=pack[low:P], in_=near[low:P])
-                nc.sync.dma_start(out=pack[0:low], in_=near[P - low : P])
+                for at, n in pieces(P - low):
+                    nc.sync.dma_start(out=pack[low + at : low + at + n], in_=near[low + at : low + at + n])
+                for at, n in pieces(low):
+                    nc.sync.dma_start(out=pack[at : at + n], in_=near[P - low + at : P - low + at + n])
                 table_of[(h, r)] = pack
 
         def regroup_v(h, g):
@@ -282,17 +288,14 @@ def tile_tnlattention_pa_kernel(tc, q, k, v, log_slope, out):
             v_codes = v_codes_of[h]
             for r in range(LAST):
                 live = (r + 1) * STEP
-                even_words = v_codes[0:live].rearrange("p (j e) d -> p e j d", e=2)
-                even_scales = v_scales[h % 2][0:live].rearrange("p (j e) d -> p e j d", e=2)
-                nc.sync.dma_start(
-                    out=v_part[h % 2][P - live : P, 0, r].bitcast(I32), in_=even_words[:, 0].bitcast(I32)
-                )
-                nc.sync.dma_start(
-                    out=vs_part[h % 2][P - live : P, r].bitcast(I32), in_=even_scales[:, 0].bitcast(I32)
-                )
-                nc.sync.dma_start(
-                    out=v_part[h % 2][0:live, 1, r].bitcast(I32), in_=even_words[:, 1].bitcast(I32)
-                )
+                for at, n in pieces(live):
+                    src = slice(at, at + n)
+                    high = slice(P - live + at, P - live + at + n)
+                    words = v_codes[src].rearrange("p (j e) d -> p e j d", e=2)
+                    scales = v_scales[h % 2][src].rearrange("p (j e) d -> p e j d", e=2)
+                    nc.sync.dma_start(out=v_part[h % 2][high, 0, r].bitcast(I32), in_=words[:, 0].bitcast(I32))
+                    nc.sync.dma_start(out=vs_part[h % 2][high, r].bitcast(I32), in_=scales[:, 0].bitcast(I32))
+                    nc.sync.dma_start(out=v_part[h % 2][src, 1, r].bitcast(I32), in_=words[:, 1].bitcast(I32))
 
         halves = [(h, i) for h in range(HEADS) for i in range(2)]
         phases = []
@@ -496,7 +499,7 @@ def tile_tnlattention_pa_kernel(tc, q, k, v, log_slope, out):
             h, i = halves[c]
             nxt = h + 1
             if i == 0:
-                if s == (4 if h > 0 else 12) and h + 2 < HEADS:
+                if s == (2 if h > 0 else 12) and h + 2 < HEADS:
                     load(h + 2, whole)
                 if h > 0:
                     if s in A_MX2:
@@ -507,10 +510,6 @@ def tile_tnlattention_pa_kernel(tc, q, k, v, log_slope, out):
                         store(h - 1, 2, 0, TILES_PER_BLOCK)
                     if s == A_O3:
                         store(h - 1, 3, 0, TILES_PER_BLOCK)
-                if h > 0:
-                    for at, what, which in A_OWN:
-                        if s == at:
-                            what_of[what](h, which)
                 if nxt < HEADS:
                     for at, what, which in A_PREP if h > 0 else A_PREP_0:
                         if s == at:
@@ -585,7 +584,12 @@ def tile_tnlattention_pa_kernel(tc, q, k, v, log_slope, out):
                 n += 1
                 for end, p in ends_of[c]:
                     if s + 1 == end:
-                        turn = (p, h if i == 0 and (end == n_steps) == (h == 0) else None)
+                        packing = None
+                        if end == n_steps and c == 0:
+                            packing = 0
+                        if end == n_steps and i == 1 and h + 1 < HEADS:
+                            packing = h + 1
+                        turn = (p, packing)
             if closing:
                 for r in range(2):
                     second_matmul(HEADS - 1, 3, r)

@@ -37,24 +37,26 @@ HELP = 5
 LIFT_BUFS = 4
 WIDEST = 17
 CODE_BUFS = 6
-A_MX2 = (1, 2, 3, 4)
-A_O2 = 4
-A_MX3 = (7, 9, 10, 11)
-A_O3 = 11
-A_PREP = ((0, "k", (0, 1)), (2, "v", 0), (5, "v", 1), (8, "q", (0, 1)), (9, "far", 0))
-A_PREP_0 = ((11, "k", (0, 1)),)
+A_MX2 = (1, 1, 2, 3)
+A_MX3 = (7, 8, 8, 9)
+A_PREP = (
+    (2, "k", (0,)), (4, "k", (1,)), (5, "near", 0), (6, "q", (1,)), (7, "v", 0), (10, "far", 0), (11, "q", (2,)),
+)
+A_PREP_0 = ((10, "k", (0,)), (12, "k", (1,)))
 B_MX0 = (1, 1, 2, 2)
-B_MX1 = (5, 6, 7, 9)
+B_MX1 = (5, 7, 8, 8)
 B_MX0_0 = (9, 9, 9, 9)
 B_MX1_0 = (11, 11, 11, 11)
-B_PREP = ((0, "q", (2, 3)), (1, "v", 2), (3, "v", 3), (4, "near", 0), (8, "k", (2, 3)))
-B_PREP_0 = (
-    (0, "q", (0, 1)), (1, "far", 0), (2, "v", 0), (3, "q", (2, 3)), (4, "v", 1), (5, "near", 0), (6, "v", 2),
-    (8, "k", (2, 3)), (9, "v", 3),
+B_PREP = (
+    (2, "q", (0,)), (3, "v", 1), (4, "q", (3,)), (5, "v", 2), (6, "k", (2,)), (7, "v", 3), (11, "k", (3,)),
 )
-LIFT_AT = ((1, 3, 6, 8), (1, 3, 6, 8))
-LIFT_0 = (5, 7, 9, 11)
-LIFT_1 = (4, 7, 8, 10)
+B_PREP_0 = (
+    (0, "q", (1,)), (1, "near", 0), (1, "q", (2,)), (2, "far", 0), (3, "q", (0,)), (4, "v", 0), (5, "q", (3,)),
+    (6, "v", 1), (7, "k", (2,)), (8, "v", 2), (9, "k", (3,)), (10, "v", 3),
+)
+LIFT_AT = ((0, 0, 8, 8, 10), (0, 0, 8, 8, 10))
+LIFT_0 = (5, 7, 9, 11, 12)
+LIFT_1 = (4, 6, 7, 8, 10)
 START_LIFT = (0, 2, 3)
 START_PREP = ((3, "k", (2, 3)), (5, "v", 0), (7, "v", 1), (9, "v", 2), (11, "v", 3))
 BANKS = 4
@@ -502,14 +504,12 @@ def tile_tnlattention_pa_kernel(tc, q, k, v, log_slope, out):
                 if s == (2 if h > 0 else 12) and h + 2 < HEADS:
                     load(h + 2, whole)
                 if h > 0:
-                    if s in A_MX2:
-                        second_matmul(h - 1, 2, A_MX2.index(s))
-                    if s in A_MX3:
-                        second_matmul(h - 1, 3, A_MX3.index(s))
-                    if s == A_O2:
-                        store(h - 1, 2, 0, TILES_PER_BLOCK)
-                    if s == A_O3:
-                        store(h - 1, 3, 0, TILES_PER_BLOCK)
+                    for b, at in ((2, A_MX2), (3, A_MX3)):
+                        for r in range(TILES_PER_BLOCK):
+                            if s == at[r]:
+                                second_matmul(h - 1, b, r)
+                        if s == at[LAST]:
+                            store(h - 1, b, 0, TILES_PER_BLOCK)
                 if nxt < HEADS:
                     for at, what, which in A_PREP if h > 0 else A_PREP_0:
                         if s == at:
@@ -574,8 +574,10 @@ def tile_tnlattention_pa_kernel(tc, q, k, v, log_slope, out):
                     for at, what, which in START_PREP:
                         if s == at:
                             what_of[what](0, which)
-                if not closing and s in lift_at:
-                    lift(first_lift + lift_at.index(s))
+                if not closing:
+                    for j in range(HELP):
+                        if s == lift_at[j]:
+                            lift(first_lift + j)
                 chore(c, s)
                 if closing and s >= n_steps - TILES_PER_BLOCK:
                     second_matmul(HEADS - 1, 2, s - n_steps + TILES_PER_BLOCK)
@@ -595,8 +597,6 @@ def tile_tnlattention_pa_kernel(tc, q, k, v, log_slope, out):
                     second_matmul(HEADS - 1, 3, r)
                     store(HEADS - 1, 3, r, r + 1)
                 break
-            for j in range(len(lift_at), HELP):
-                lift(first_lift + j)
             if c == 0:
                 zero_set(1)
         last = len(phases) - 1

@@ -51,9 +51,9 @@ B_PREP = (
     (2, "q", (0,)), (3, "v", 1), (4, "q", (3,)), (5, "v", 2), (6, "k", (2,)), (7, "v", 3), (11, "k", (3,)),
 )
 B_PREP_0 = (
-    (0, "q", (1,)), (1, "near", 0), (1, "q", (2,)), (2, "far", 0), (3, "q", (0,)), (4, "v", 0), (5, "q", (3,)),
-    (6, "v", 1), (7, "k", (2,)), (8, "v", 2), (9, "k", (3,)), (10, "v", 3),
+    (0, "q", (1,)), (1, "near", 0), (1, "q", (2,)), (2, "far", 0), (3, "q", (0,)), (5, "q", (3,)), (7, "k", (2,)), (9, "k", (3,)),
 )
+A_OWN_1 = ((0, "v", 0), (1, "v", 1), (3, "v", 2), (5, "v", 3))
 LIFT_AT = ((0, 0, 8, 8, 10), (0, 0, 8, 8, 10))
 LIFT_0 = (5, 7, 9, 11, 12)
 LIFT_1 = (4, 6, 7, 8, 10)
@@ -68,14 +68,10 @@ OPENING = (
     + [("pack", 0, r) for r in range(LAST)]
 )
 FIRST = [
-    ("far", 1, 0, 0), ("pack", 0, 0), ("far", 1, 0, 1), ("far", 1, 0, 2), ("pack", 0, 1), ("near", 0), ("near", 1),
-    ("pack", 0, 2), ("far", 2, 0, 1), ("far", 2, 0, 3), ("far", 2, 1, 1), ("far", 2, 1, 3),
-    ("far", 1, 0, 3), ("far", 2, 0, 0), ("far", 2, 0, 2), ("far", 2, 1, 0), ("far", 2, 1, 2),
+    ("pack", 0, 0), ("far", 1, 0, 0), ("pack", 0, 1), ("far", 1, 0, 1), ("far", 1, 0, 2), ("near", 0), ("near", 1), ("pack", 0, 2), ("far", 2, 0, 1), ("far", 2, 0, 3), ("far", 2, 1, 1), ("far", 2, 1, 3), ("far", 1, 0, 3), ("far", 2, 0, 0), ("far", 2, 0, 2), ("far", 2, 1, 0), ("far", 2, 1, 2),
 ]
 SECOND = [
-    ("far", 3, 0, 0), ("pack", 1, 0), ("far", 3, 0, 2), ("far", 3, 1, 0), ("pack", 1, 1), ("near", 2), ("near", 3),
-    ("pack", 1, 2), ("far", 3, 1, 2), ("far", 3, 2, 0), ("far", 3, 2, 2), ("far", 3, 2, 3),
-    ("far", 3, 0, 1), ("far", 3, 0, 3), ("far", 3, 1, 1), ("far", 3, 1, 3), ("far", 3, 2, 1),
+    ("pack", 1, 0), ("far", 3, 0, 0), ("pack", 1, 1), ("far", 3, 0, 2), ("far", 3, 1, 0), ("near", 2), ("near", 3), ("pack", 1, 2), ("far", 3, 1, 2), ("far", 3, 2, 0), ("far", 3, 2, 2), ("far", 3, 2, 3), ("far", 3, 0, 1), ("far", 3, 0, 3), ("far", 3, 1, 1), ("far", 3, 1, 3), ("far", 3, 2, 1),
 ]
 CLOSING = [
     ("pack", 1, 0), ("far", 3, 0, 1), ("pack", 1, 1), ("far", 3, 1, 1), ("pack", 1, 2), ("far", 3, 2, 1), ("near", 2),
@@ -384,7 +380,7 @@ def tile_tnlattention_pa_kernel(tc, q, k, v, log_slope, out):
 
         def multiply(n):
             p, slot, h, tile = direct_tiles[n]
-            if slot == 0:
+            if p not in energy_of:
                 energy = work.tile([P, phases[p][2], P, PACK], BF16, align_bytes=64)
                 energy_of[p] = energy
             s_view = bank_of[n][:].rearrange("p t c -> p c t")
@@ -501,7 +497,7 @@ def tile_tnlattention_pa_kernel(tc, q, k, v, log_slope, out):
             h, i = halves[c]
             nxt = h + 1
             if i == 0:
-                if s == (2 if h > 0 else 12) and h + 2 < HEADS:
+                if s == (12, 10, 2)[min(h, 2)] and h + 2 < HEADS:
                     load(h + 2, whole)
                 if h > 0:
                     for b, at in ((2, A_MX2), (3, A_MX3)):
@@ -510,12 +506,16 @@ def tile_tnlattention_pa_kernel(tc, q, k, v, log_slope, out):
                                 second_matmul(h - 1, b, r)
                         if s == at[LAST]:
                             store(h - 1, b, 0, TILES_PER_BLOCK)
+                if h == 1:
+                    for at, what, which in A_OWN_1:
+                        if s == at:
+                            what_of[what](h, which)
                 if nxt < HEADS:
                     for at, what, which in A_PREP if h > 0 else A_PREP_0:
                         if s == at:
                             what_of[what](nxt, which)
             else:
-                for b, at in enumerate((B_MX0, B_MX1) if h > 0 else (B_MX0_0, B_MX1_0)):
+                for b, at in enumerate((B_MX0, B_MX1) if h > 1 else (B_MX0_0, B_MX1_0)):
                     for r in range(TILES_PER_BLOCK):
                         if s == at[r]:
                             second_matmul(h, b, r)
@@ -546,6 +546,12 @@ def tile_tnlattention_pa_kernel(tc, q, k, v, log_slope, out):
         fill(3)
         lift(0)
         flip_q(0, (2, 3), 2)
+        order = []
+        for first, helped_first, n_direct, n_helped in phases:
+            at = first + (min(BANKS, n_direct - 1) if first > 0 else 1)
+            order += [first, at] + [m for m in range(first + 1, first + n_direct) if m != at]
+        multiplied = set()
+        n_filled = BANKS
         n = 0
         turn = None
         for c in range(len(halves)):
@@ -555,7 +561,8 @@ def tile_tnlattention_pa_kernel(tc, q, k, v, log_slope, out):
             n_steps = ends_of[c][-1][0]
             first_lift = phases[ends_of[c][-1][1]][1] + phases[ends_of[c][-1][1]][3]
             for s in range(n_steps):
-                multiply(n)
+                multiply(order[n])
+                multiplied.add(order[n])
                 if turn is not None:
                     if turn[1] is not None:
                         quantise_v(turn[1])
@@ -563,8 +570,9 @@ def tile_tnlattention_pa_kernel(tc, q, k, v, log_slope, out):
                     quantise_phase(turn[0])
                     help_phase(turn[0] + 1)
                     turn = None
-                if n + BANKS < len(direct_tiles):
-                    fill(n + BANKS)
+                while n_filled < len(direct_tiles) and n_filled - BANKS in multiplied:
+                    fill(n_filled)
+                    n_filled += 1
                 if c == 0:
                     if s in START_LIFT:
                         m = 1 + START_LIFT.index(s)
@@ -587,9 +595,9 @@ def tile_tnlattention_pa_kernel(tc, q, k, v, log_slope, out):
                 for end, p in ends_of[c]:
                     if s + 1 == end:
                         packing = None
-                        if end == n_steps and c == 0:
-                            packing = 0
-                        if end == n_steps and i == 1 and h + 1 < HEADS:
+                        if (end == n_steps and c == 0) or (end < n_steps and c == 2):
+                            packing = h
+                        if end == n_steps and i == 1 and 0 < h < HEADS - 1:
                             packing = h + 1
                         turn = (p, packing)
             if closing:

@@ -29,7 +29,7 @@ TINY = 2.0**-60
 
 FLOPS = 2 * 2 * HEADS * HEAD_DIM * BLOCK * BLOCK * (N_BLOCKS * (N_BLOCKS + 1) // 2)
 
-SPLIT = ((8, 4), (4, 1))
+SPLIT = ((7, 3), (5, 2))
 OPEN = ((8, 2), (5, 2))
 PHASES = {"opening": OPEN, "first": SPLIT, "second": SPLIT, "closing": SPLIT}
 DIRECT = 12
@@ -42,7 +42,7 @@ A_MX3 = (7, 8, 8, 9)
 A_PREP = (
     (2, "k", (0,)), (4, "k", (1,)), (5, "near", 0), (6, "q", (1,)), (7, "v", 0), (10, "far", 0), (11, "q", (2,)),
 )
-A_PREP_0 = ((10, "k", (0,)), (12, "k", (1,)))
+A_PREP_0 = ((8, "near", 0), (10, "k", (0,)), (12, "k", (1,)))
 B_MX0 = (1, 1, 2, 2)
 B_MX1 = (5, 7, 8, 8)
 B_MX0_0 = (9, 9, 9, 9)
@@ -51,14 +51,14 @@ B_PREP = (
     (2, "q", (0,)), (3, "v", 1), (4, "q", (3,)), (5, "v", 2), (6, "k", (2,)), (7, "v", 3), (11, "k", (3,)),
 )
 B_PREP_0 = (
-    (0, "q", (1,)), (1, "near", 0), (1, "q", (2,)), (2, "far", 0), (3, "q", (0,)), (5, "q", (3,)), (7, "k", (2,)), (9, "k", (3,)),
+    (0, "q", (1,)), (1, "q", (2,)), (2, "far", 0), (3, "q", (0,)), (5, "q", (3,)), (7, "k", (2,)), (8, "v", 0), (9, "k", (3,)), (10, "v", 1),
 )
-A_OWN_1 = ((0, "v", 0), (1, "v", 1), (3, "v", 2), (5, "v", 3))
-LIFT_AT = ((0, 0, 8, 8, 10), (0, 0, 8, 8, 10))
+A_OWN_1 = ((1, "v", 2), (3, "v", 3))
+LIFT_AT = ((0, 0, 7, 7, 9), (0, 0, 7, 7, 9))
 LIFT_0 = (5, 7, 9, 11, 12)
 LIFT_1 = (4, 6, 7, 8, 10)
 START_LIFT = (0, 2, 3)
-START_PREP = ((3, "k", (2, 3)), (5, "v", 0), (7, "v", 1), (9, "v", 2), (11, "v", 3))
+START_PREP = ((3, "k", (2, 3)), (4, "v", 0), (5, "v", 1), (6, "v", 2), (8, "v", 3))
 BANKS = 4
 
 OPENING = (
@@ -134,7 +134,6 @@ def tile_tnlattention_pa_kernel(tc, q, k, v, log_slope, out):
         nc.vector.memset(slope_row[:], 0.0)
         nc.sync.dma_start(out=slope_row[0:1], in_=log_slope.rearrange("(a h) -> a h", a=1))
         load(0, [("k", 0, 1), ("q", 1, 2), ("k", 1, 2), ("q", 0, 1), ("q", 2, 4), ("k", 2, 4), ("v", 0, 4)])
-        load(1, whole)
         warm = const.tile([P, 1], F32)
         nc.vector.memset(warm[:], 0.0)
         warmed = const.tile([P, 1], F32)
@@ -142,13 +141,12 @@ def tile_tnlattention_pa_kernel(tc, q, k, v, log_slope, out):
         ones = const.tile([P, P], BF16)
         nc.vector.memset(ones[:], 1.0)
 
-        ident = const.tile([P, P], BF16)
-        make_identity(nc, ident[:])
-
         dist_int = const.tile([P, P, PACK], I32)
         nc.gpsimd.iota(dist_int[:], pattern=[[1, P], [-1, PACK]], base=LAST * P, channel_multiplier=-PACK)
         step_int = const.tile([P, FAR_STEPS], I32)
         nc.gpsimd.iota(step_int[:], pattern=[[P, FAR_STEPS]], base=0, channel_multiplier=0)
+        ident = const.tile([P, P], BF16)
+        make_identity(nc, ident[:])
 
         k_even_a = const.tile([P, N_PAIRS, PACK, LAST * STEP + P], BF16, align_bytes=64)
         k_even_b = const.tile([P, N_PAIRS, PACK, LAST * STEP + P], BF16, align_bytes=64)
@@ -175,13 +173,11 @@ def tile_tnlattention_pa_kernel(tc, q, k, v, log_slope, out):
             nc.gpsimd.memset(v_scales[i][:].bitcast(U32), 0)
 
         zero_set(0)
+        zero_set(1)
 
         l_bank = psum_l.tile([P, HEADS], F32)
         nc.tensor.matmul(l_bank[:], lhsT=ones[:], rhs=slope_row[:], start=True, stop=True)
         slope = const.tile([P, HEADS], F32)
-        nc.vector.tensor_scalar_min(out=slope[:], in0=l_bank[:], scalar1=-TINY)
-        slope_tile = const.tile([P, HEADS], F32)
-        nc.vector.tensor_scalar_mul(out=slope_tile[:], in0=slope[:], scalar1=float(P))
         dist = const.tile([P, P, PACK], F32)
         nc.vector.tensor_copy(out=dist[:], in_=dist_int[:])
         step = const.tile([P, FAR_STEPS], F32)
@@ -190,6 +186,9 @@ def tile_tnlattention_pa_kernel(tc, q, k, v, log_slope, out):
         nc.vector.scalar_tensor_tensor(
             out=causal[:], in0=dist[:], scalar=-FOREVER, in1=dist[:], op0=ALU.mult, op1=ALU.max
         )
+        nc.vector.tensor_scalar_min(out=slope[:], in0=l_bank[:], scalar1=-TINY)
+        slope_tile = const.tile([P, HEADS], F32)
+        nc.vector.tensor_scalar_mul(out=slope_tile[:], in0=slope[:], scalar1=float(P))
         q_cols_of = {}
         k_odd_of = {}
         table_of = {}
@@ -213,13 +212,17 @@ def tile_tnlattention_pa_kernel(tc, q, k, v, log_slope, out):
                     nc.tensor.transpose(flipped[:, i * PACK + j, :], tiles[:, j, :], ident[:])
             return flipped
 
-        def flip_q(h, blocks, early=0):
+        def flip_q(h, blocks, early=0, by_vector=False):
             if h not in q_cols_of:
                 q_cols = head.tile([P, N_BLOCKS * TILES_PER_BLOCK, P], BF16)
                 q_cols_of[h] = q_cols
             flipped = flip([rows_of[h][1][:, b] for b in blocks], early)
             first = blocks[0] * TILES_PER_BLOCK
-            nc.scalar.copy(out=q_cols_of[h][:, first : first + TILES_PER_BLOCK * len(blocks)], in_=flipped[:])
+            dst = q_cols_of[h][:, first : first + TILES_PER_BLOCK * len(blocks)]
+            if by_vector:
+                nc.vector.tensor_copy(out=dst, in_=flipped[:])
+            else:
+                nc.scalar.copy(out=dst, in_=flipped[:])
 
         def flip_k(h, groups, early=0):
             if h not in k_odd_of:
@@ -271,7 +274,8 @@ def tile_tnlattention_pa_kernel(tc, q, k, v, log_slope, out):
             if g == 0:
                 v_grouped = head.tile([P, N_BLOCKS, HEAD_DIM, PACK], BF16, align_bytes=64)
                 v_grouped_of[h] = v_grouped
-            nc.scalar.copy(out=v_grouped_of[h][:, g], in_=rows_of[h][2][:, g].rearrange("p t d -> p d t"))
+            src = rows_of[h][2][:, g].rearrange("p t d -> p d t")
+            nc.scalar.copy(out=v_grouped_of[h][:, g], in_=src)
 
         def quantise_v(h):
             v_codes = head.tile([P, N_BLOCKS, HEAD_DIM], U32, align_bytes=64)
@@ -497,7 +501,9 @@ def tile_tnlattention_pa_kernel(tc, q, k, v, log_slope, out):
             h, i = halves[c]
             nxt = h + 1
             if i == 0:
-                if s == (12, 10, 2)[min(h, 2)] and h + 2 < HEADS:
+                if h == 0 and s == 3:
+                    load(1, whole)
+                if h > 0 and s == (10, 2)[min(h, 2) - 1] and h + 2 < HEADS:
                     load(h + 2, whole)
                 if h > 0:
                     for b, at in ((2, A_MX2), (3, A_MX3)):
@@ -515,6 +521,8 @@ def tile_tnlattention_pa_kernel(tc, q, k, v, log_slope, out):
                         if s == at:
                             what_of[what](nxt, which)
             else:
+                if h == 0 and s == 5:
+                    load(2, whole)
                 for b, at in enumerate((B_MX0, B_MX1) if h > 1 else (B_MX0_0, B_MX1_0)):
                     for r in range(TILES_PER_BLOCK):
                         if s == at[r]:
@@ -535,20 +543,20 @@ def tile_tnlattention_pa_kernel(tc, q, k, v, log_slope, out):
         }
 
         flip_k(0, (0,), 1)
-        flip_q(0, (1,), 2)
         decay_far(0)
+        flip_q(0, (1,), 2)
+        flip_k(0, (1,), 1)
+        flip_q(0, (0,), by_vector=True)
+        decay_near(0)
         fill(0)
         fill(1)
-        flip_k(0, (1,))
-        decay_near(0)
-        flip_q(0, (0,), 2)
         fill(2)
         fill(3)
         lift(0)
         flip_q(0, (2, 3), 2)
         order = []
         for first, helped_first, n_direct, n_helped in phases:
-            at = first + (min(BANKS, n_direct - 1) if first > 0 else 1)
+            at = first + (min(BANKS, n_direct) - 1 if first > 0 else 1)
             order += [first, at] + [m for m in range(first + 1, first + n_direct) if m != at]
         multiplied = set()
         n_filled = BANKS
@@ -605,8 +613,6 @@ def tile_tnlattention_pa_kernel(tc, q, k, v, log_slope, out):
                     second_matmul(HEADS - 1, 3, r)
                     store(HEADS - 1, 3, r, r + 1)
                 break
-            if c == 0:
-                zero_set(1)
         last = len(phases) - 1
         quantise(last, helped_of[last][:], phases[last][2])
         quantise(last, energy_of[last][:].rearrange("p s c t -> p s (c t)"), 0)

@@ -40,25 +40,25 @@ CODE_BUFS = 6
 A_MX2 = (1, 1, 2, 3)
 A_MX3 = (7, 8, 8, 9)
 A_PREP = (
-    (2, "k", (0,)), (4, "k", (1,)), (5, "near", 0), (6, "q", (1,)), (7, "v", 0), (10, "far", 0), (11, "q", (2,)),
+    (2, "k", (0,)), (4, "k", (1,)), (5, "own", LAST), (6, "q", (1,)), (7, "v", 0), (8, "own", 0), (9, "own", 1), (10, "far", 0), (11, "q", (2,)),
 )
-A_PREP_0 = ((8, "near", 0), (10, "k", (0,)), (12, "k", (1,)))
+A_PREP_0 = ((8, "own", LAST), (9, "own", 0), (10, "k", (0,)), (12, "k", (1,)))
 B_MX0 = (1, 1, 2, 2)
 B_MX1 = (5, 7, 8, 8)
 B_MX0_0 = (9, 9, 9, 9)
 B_MX1_0 = (11, 11, 11, 11)
 B_PREP = (
-    (2, "q", (0,)), (3, "v", 1), (4, "q", (3,)), (5, "v", 2), (6, "k", (2,)), (7, "v", 3), (11, "k", (3,)),
+    (1, "own", 2), (2, "q", (0,)), (3, "v", 1), (4, "q", (3,)), (5, "v", 2), (6, "k", (2,)), (7, "v", 3), (11, "k", (3,)),
 )
 B_PREP_0 = (
-    (0, "q", (1,)), (1, "q", (2,)), (2, "far", 0), (3, "q", (0,)), (5, "q", (3,)), (7, "k", (2,)), (8, "v", 0), (9, "k", (3,)), (10, "v", 1),
+    (0, "q", (1,)), (1, "q", (2,)), (1, "own", 1), (2, "far", 0), (3, "own", 2), (3, "q", (0,)), (5, "q", (3,)), (7, "k", (2,)), (8, "v", 0), (9, "k", (3,)), (10, "v", 1),
 )
 A_OWN_1 = ((1, "v", 2), (3, "v", 3))
 LIFT_AT = ((0, 0, 7, 7, 9), (0, 0, 7, 7, 9))
 LIFT_0 = (5, 7, 9, 11, 12)
 LIFT_1 = (4, 6, 7, 8, 10)
 START_LIFT = (0, 2, 3)
-START_PREP = ((3, "k", (2, 3)), (4, "v", 0), (5, "v", 1), (6, "v", 2), (8, "v", 3))
+START_PREP = ((3, "k", (2, 3)), (4, "own", 0), (5, "own", 1), (6, "v", 0), (7, "own", 2), (8, "v", 1), (9, "v", 2), (10, "v", 3))
 BANKS = 4
 
 OPENING = (
@@ -186,6 +186,10 @@ def tile_tnlattention_pa_kernel(tc, q, k, v, log_slope, out):
         nc.vector.scalar_tensor_tensor(
             out=causal[:], in0=dist[:], scalar=-FOREVER, in1=dist[:], op0=ALU.mult, op1=ALU.max
         )
+        pack_0 = const.tile([P, P, PACK], F32)
+        pack_1 = const.tile([P, P, PACK], F32)
+        pack_2 = const.tile([P, P, PACK], F32)
+        own_dist = [pack_0, pack_1, pack_2, causal]
         nc.vector.tensor_scalar_min(out=slope[:], in0=l_bank[:], scalar1=-TINY)
         slope_tile = const.tile([P, HEADS], F32)
         nc.vector.tensor_scalar_mul(out=slope_tile[:], in0=slope[:], scalar1=float(P))
@@ -257,18 +261,10 @@ def tile_tnlattention_pa_kernel(tc, q, k, v, log_slope, out):
             nc.scalar.activation(out=far_step[:], in_=step[:], func=ACT.Exp, scale=slope_h)
             far_step_of[h] = far_step
 
-        def decay_near(h):
-            near = head.tile([P, P, PACK], F32)
-            nc.scalar.activation(out=near[:], in_=causal[:], func=ACT.Exp, scale=slope[:, h : h + 1])
-            table_of[(h, LAST)] = near
-            for r in range(LAST):
-                pack = head.tile([P, P, PACK], F32, bufs=2 * LAST)
-                low = (LAST - r) * STEP
-                for at, n in pieces(P - low):
-                    nc.sync.dma_start(out=pack[low + at : low + at + n], in_=near[low + at : low + at + n])
-                for at, n in pieces(low):
-                    nc.sync.dma_start(out=pack[at : at + n], in_=near[P - low + at : P - low + at + n])
-                table_of[(h, r)] = pack
+        def decay_own(h, r):
+            own = head.tile([P, P, PACK], F32, bufs=2 * TILES_PER_BLOCK)
+            nc.scalar.activation(out=own[:], in_=own_dist[r][:], func=ACT.Exp, scale=slope[:, h : h + 1])
+            table_of[(h, r)] = own
 
         def regroup_v(h, g):
             if g == 0:
@@ -539,7 +535,7 @@ def tile_tnlattention_pa_kernel(tc, q, k, v, log_slope, out):
             "q": flip_q,
             "v": regroup_v,
             "far": lambda h, which: decay_far(h),
-            "near": lambda h, which: decay_near(h),
+            "own": decay_own,
         }
 
         flip_k(0, (0,), 1)
@@ -547,7 +543,13 @@ def tile_tnlattention_pa_kernel(tc, q, k, v, log_slope, out):
         flip_q(0, (1,), 2)
         flip_k(0, (1,), 1)
         flip_q(0, (0,), by_vector=True)
-        decay_near(0)
+        decay_own(0, LAST)
+        for r in range(LAST):
+            low = (LAST - r) * STEP
+            for at, n in pieces(P - low):
+                nc.sync.dma_start(out=own_dist[r][low + at : low + at + n], in_=causal[low + at : low + at + n])
+            for at, n in pieces(low):
+                nc.sync.dma_start(out=own_dist[r][at : at + n], in_=causal[P - low + at : P - low + at + n])
         fill(0)
         fill(1)
         fill(2)

@@ -37,29 +37,26 @@ HELP = 5
 LIFT_BUFS = 4
 WIDEST = 17
 CODE_BUFS = 6
-A_MX2 = (1, 1, 2, 3)
-A_MX3 = (7, 8, 8, 9)
-A_PREP = (
-    (2, "k", (0,)), (4, "k", (1,)), (5, "own", LAST), (6, "q", (1,)), (7, "v", 0), (8, "own", 0), (9, "own", 1), (10, "far", 0), (11, "q", (2,)),
+OUT_AT = ((0, 7), (0, 7))
+OUT_CLOSE = (4, 6)
+FIRST_LOADS = (3, 5)
+LOAD_AT = 1
+OWN = (((1, "v", 2), (3, "v", 3)), ())
+OWN_0 = ((), ((1, "v", 2), (3, "v", 3)))
+NEXT = (
+    ((2, "k", (0,)), (4, "k", (1,)), (6, "q", (1,)), (8, "own", LAST), (9, "q", (2,)), (10, "far", 0)),
+    ((1, "own", 0), (2, "q", (0,)), (3, "own", 1), (4, "q", (3,)), (5, "v", 0), (6, "own", 2), (9, "k", (2,)), (10, "v", 1), (11, "k", (3,))),
 )
-A_PREP_0 = ((8, "own", LAST), (9, "own", 0), (10, "k", (0,)), (12, "k", (1,)))
-B_MX0 = (1, 1, 2, 2)
-B_MX1 = (5, 7, 8, 8)
-B_MX0_0 = (9, 9, 9, 9)
-B_MX1_0 = (11, 11, 11, 11)
-B_PREP = (
-    (1, "own", 2), (2, "q", (0,)), (3, "v", 1), (4, "q", (3,)), (5, "v", 2), (6, "k", (2,)), (7, "v", 3), (11, "k", (3,)),
+NEXT_0 = (
+    ((8, "own", LAST), (10, "k", (0,)), (11, "own", 0), (12, "k", (1,))),
+    ((0, "q", (1,)), (1, "far", 0), (2, "q", (0,)), (3, "own", 1), (4, "q", (2,)), (5, "own", 2), (6, "k", (2,)), (8, "q", (3,)), (9, "v", 0), (10, "k", (3,)), (11, "v", 1)),
 )
-B_PREP_0 = (
-    (0, "q", (1,)), (1, "q", (2,)), (1, "own", 1), (2, "far", 0), (3, "own", 2), (3, "q", (0,)), (5, "q", (3,)), (7, "k", (2,)), (8, "v", 0), (9, "k", (3,)), (10, "v", 1),
-)
-A_OWN_1 = ((1, "v", 2), (3, "v", 3))
-LIFT_AT = ((0, 0, 7, 7, 9), (0, 0, 7, 7, 9))
+LIFT_AT = ((0, 1, 5, 7, 9), (0, 1, 5, 7, 9))
 LIFT_0 = (5, 7, 9, 11, 12)
 LIFT_1 = (4, 6, 7, 8, 10)
 START_LIFT = (0, 2, 3)
-START_PREP = ((3, "k", (2, 3)), (4, "own", 0), (5, "own", 1), (6, "v", 0), (7, "own", 2), (8, "v", 1), (9, "v", 2), (10, "v", 3))
-BANKS = 4
+START_PREP = ((3, "k", (2, 3)), (4, "own", 0), (5, "own", 1), (6, "own", 2), (9, "v", 0), (10, "v", 1))
+BANKS = 5
 
 OPENING = (
     [("far", 1, 0, r) for r in range(TILES_PER_BLOCK)]
@@ -112,7 +109,6 @@ def tile_tnlattention_pa_kernel(tc, q, k, v, log_slope, out):
         psum_s = ctx.enter_context(tc.psum_pool(name="psum_s", bufs=BANKS))
         psum_l = ctx.enter_context(tc.psum_pool(name="psum_l", bufs=2))
         psum_o = ctx.enter_context(tc.psum_pool(name="psum_o", bufs=1))
-        psum_t = ctx.enter_context(tc.psum_pool(name="psum_t", bufs=1))
         ctx.enter_context(tc.manual_schedule())
 
         rows_of = {}
@@ -206,11 +202,11 @@ def tile_tnlattention_pa_kernel(tc, q, k, v, log_slope, out):
                 s_bank = psum_s.tile([P, n_tiles, P], BF16)
                 flipped = s_bank
             elif early == 2:
+                l_bank = psum_l.tile([P, n_tiles, P], BF16)
+                flipped = l_bank
+            else:
                 o_bank = psum_o.tile([P, n_tiles, P], BF16)
                 flipped = o_bank
-            else:
-                t_bank = psum_t.tile([P, n_tiles, P], BF16)
-                flipped = t_bank
             for i, tiles in enumerate(row_tiles):
                 for j in range(PACK):
                     nc.tensor.transpose(flipped[:, i * PACK + j, :], tiles[:, j, :], ident[:])
@@ -495,40 +491,25 @@ def tile_tnlattention_pa_kernel(tc, q, k, v, log_slope, out):
 
         def chore(c, s):
             h, i = halves[c]
-            nxt = h + 1
-            if i == 0:
-                if h == 0 and s == 3:
-                    load(1, whole)
-                if h > 0 and s == (10, 2)[min(h, 2) - 1] and h + 2 < HEADS:
-                    load(h + 2, whole)
-                if h > 0:
-                    for b, at in ((2, A_MX2), (3, A_MX3)):
-                        for r in range(TILES_PER_BLOCK):
-                            if s == at[r]:
-                                second_matmul(h - 1, b, r)
-                        if s == at[LAST]:
-                            store(h - 1, b, 0, TILES_PER_BLOCK)
-                if h == 1:
-                    for at, what, which in A_OWN_1:
-                        if s == at:
-                            what_of[what](h, which)
-                if nxt < HEADS:
-                    for at, what, which in A_PREP if h > 0 else A_PREP_0:
-                        if s == at:
-                            what_of[what](nxt, which)
-            else:
-                if h == 0 and s == 5:
-                    load(2, whole)
-                for b, at in enumerate((B_MX0, B_MX1) if h > 1 else (B_MX0_0, B_MX1_0)):
+            if h == 0 and s == FIRST_LOADS[i]:
+                load(1 + i, whole)
+            if 0 < h < HEADS - 2 and i == 1 and s == LOAD_AT:
+                load(h + 2, whole)
+            due = [(h - 1, 2 * i + b, at) for b, at in enumerate(OUT_AT[i])] if h > 0 else []
+            if c + 1 == len(halves):
+                due += [(h, b, at) for b, at in enumerate(OUT_CLOSE)]
+            for of, b, at in due:
+                if s == at:
                     for r in range(TILES_PER_BLOCK):
-                        if s == at[r]:
-                            second_matmul(h, b, r)
-                    if s == at[LAST]:
-                        store(h, b, 0, TILES_PER_BLOCK)
-                if nxt < HEADS:
-                    for at, what, which in B_PREP if h > 0 else B_PREP_0:
-                        if s == at:
-                            what_of[what](nxt, which)
+                        second_matmul(of, b, r)
+                    store(of, b, 0, TILES_PER_BLOCK)
+            for at, what, which in OWN_0[i] if h == 0 else OWN[i]:
+                if s == at:
+                    what_of[what](h, which)
+            if h + 1 < HEADS:
+                for at, what, which in NEXT_0[i] if h == 0 else NEXT[i]:
+                    if s == at:
+                        what_of[what](h + 1, which)
 
         what_of = {
             "k": flip_k,
@@ -554,12 +535,17 @@ def tile_tnlattention_pa_kernel(tc, q, k, v, log_slope, out):
         fill(1)
         fill(2)
         fill(3)
+        fill(4)
         lift(0)
         flip_q(0, (2, 3), 2)
         order = []
         for first, helped_first, n_direct, n_helped in phases:
             at = first + (min(BANKS, n_direct) - 1 if first > 0 else 1)
-            order += [first, at] + [m for m in range(first + 1, first + n_direct) if m != at]
+            rest = [m for m in range(first + 1, first + n_direct) if m != at]
+            if first > 0:
+                tail = rest[BANKS - 2 :]
+                rest = rest[: BANKS - 2] + [m for i in range(0, len(tail), 2) for m in reversed(tail[i : i + 2])]
+            order += [first, at] + rest
         multiplied = set()
         n_filled = BANKS
         n = 0
@@ -605,10 +591,8 @@ def tile_tnlattention_pa_kernel(tc, q, k, v, log_slope, out):
                 for end, p in ends_of[c]:
                     if s + 1 == end:
                         packing = None
-                        if (end == n_steps and c == 0) or (end < n_steps and c == 2):
+                        if (end == n_steps and i == 0 and h > 0) or (end < n_steps and c == 1):
                             packing = h
-                        if end == n_steps and i == 1 and 0 < h < HEADS - 1:
-                            packing = h + 1
                         turn = (p, packing)
             if closing:
                 for r in range(2):

from contextlib import ExitStack

import concourse.mybir as mybir
from concourse.masks import make_identity

F32 = mybir.dt.float32
BF16 = mybir.dt.bfloat16
I32 = mybir.dt.int32
U32 = mybir.dt.uint32
U8 = mybir.dt.uint8
FP8X4 = mybir.dt.float8_e4m3fn_x4
ALU = mybir.AluOpType
ACT = mybir.ActivationFunctionType

P = 128
PACK = 4
HEADS = 8
SEQ = 2048
HEAD_DIM = 128
BLOCK = 512
N_BLOCKS = SEQ // BLOCK
TILES_PER_BLOCK = BLOCK // P
N_PAIRS = N_BLOCKS // 2
LAST = TILES_PER_BLOCK - 1
STEP = P // PACK
FAR_STEPS = (N_BLOCKS - 1) * TILES_PER_BLOCK
FOREVER = 2.0**100
TINY = 2.0**-60

FLOPS = 2 * 2 * HEADS * HEAD_DIM * BLOCK * BLOCK * (N_BLOCKS * (N_BLOCKS + 1) // 2)

SPLIT = ((7, 3), (5, 2))
OPEN = ((8, 2), (5, 2))
PHASES = {"opening": OPEN, "first": SPLIT, "second": SPLIT, "closing": SPLIT}
DIRECT = 12
HELP = 5
LIFT_BUFS = 4
WIDEST = 17
CODE_BUFS = 6
OUT_AT = ((0, 7), (0, 7))
OUT_CLOSE = (4, 6)
FIRST_LOADS = (3, 5)
LOAD_AT = 1
OWN = (((1, "v", 2), (3, "v", 3)), ())
OWN_0 = ((), ((1, "v", 2), (3, "v", 3)))
NEXT = (
    ((2, "k", (0,)), (4, "k", (1,)), (6, "q", (1,)), (8, "own", LAST), (9, "q", (2,)), (10, "far", 0)),
    ((1, "own", 0), (2, "q", (0,)), (3, "own", 1), (4, "q", (3,)), (5, "v", 0), (6, "own", 2), (9, "k", (2,)), (10, "v", 1), (11, "k", (3,))),
)
NEXT_0 = (
    ((8, "own", LAST), (10, "k", (0,)), (11, "own", 0), (12, "k", (1,))),
    ((0, "q", (1,)), (1, "far", 0), (2, "q", (0,)), (3, "own", 1), (4, "q", (2,)), (5, "own", 2), (6, "k", (2,)), (8, "q", (3,)), (9, "v", 0), (10, "k", (3,)), (11, "v", 1)),
)
LIFT_AT = ((0, 1, 5, 7, 9), (0, 1, 5, 7, 9))
LIFT_0 = (5, 7, 9, 11, 12)
LIFT_1 = (4, 6, 7, 8, 10)
START_LIFT = (0, 2, 3)
START_PREP = ((3, "k", (2, 3)), (4, "own", 0), (5, "own", 1), (6, "own", 2), (9, "v", 0), (10, "v", 1))
BANKS = 5

OPENING = (
    [("far", 1, 0, r) for r in range(TILES_PER_BLOCK)]
    + [("near", 0), ("near", 1)]
    + [("far", 2, g, r) for g in range(2) for r in range(TILES_PER_BLOCK)]
    + [("pack", 0, r) for r in range(LAST)]
)
FIRST = [
    ("pack", 0, 0), ("far", 1, 0, 0), ("pack", 0, 1), ("far", 1, 0, 1), ("far", 1, 0, 2), ("near", 0), ("near", 1), ("pack", 0, 2), ("far", 2, 0, 1), ("far", 2, 0, 3), ("far", 2, 1, 1), ("far", 2, 1, 3), ("far", 1, 0, 3), ("far", 2, 0, 0), ("far", 2, 0, 2), ("far", 2, 1, 0), ("far", 2, 1, 2),
]
SECOND = [
    ("pack", 1, 0), ("far", 3, 0, 0), ("pack", 1, 1), ("far", 3, 0, 2), ("far", 3, 1, 0), ("near", 2), ("near", 3), ("pack", 1, 2), ("far", 3, 1, 2), ("far", 3, 2, 0), ("far", 3, 2, 2), ("far", 3, 2, 3), ("far", 3, 0, 1), ("far", 3, 0, 3), ("far", 3, 1, 1), ("far", 3, 1, 3), ("far", 3, 2, 1),
]
CLOSING = [
    ("pack", 1, 0), ("far", 3, 0, 1), ("pack", 1, 1), ("far", 3, 1, 1), ("pack", 1, 2), ("far", 3, 2, 1), ("near", 2),
    ("far", 3, 0, 2), ("far", 3, 0, 3), ("far", 3, 1, 3), ("far", 3, 2, 3), ("near", 3),
    ("far", 3, 0, 0), ("far", 3, 1, 0), ("far", 3, 2, 0), ("far", 3, 1, 2), ("far", 3, 2, 2),
]
HELPED = {
    "opening": [("far", 1, 0, 3), ("far", 2, 0, 0), ("far", 2, 0, 2), ("far", 2, 1, 0)],
    "first": FIRST[DIRECT:],
    "second": SECOND[DIRECT:],
    "closing": CLOSING[DIRECT:],
}


def widths(n):
    runs = []
    at = 0
    while at < n:
        w = 8
        while w > n - at:
            w //= 2
        runs.append((at, w))
        at += w
    return runs


def pieces(n):
    return ([(0, 64)] if n >= 64 else []) + ([(n // 64 * 64, 32)] if n % 64 else [])


def tile_tnlattention_pa_kernel(tc, q, k, v, log_slope, out):
    nc = tc.nc
    with ExitStack() as ctx:
        const = ctx.enter_context(tc.tile_pool(name="const", bufs=1))
        rows = ctx.enter_context(tc.tile_pool(name="rows", bufs=2))
        head = ctx.enter_context(tc.tile_pool(name="head", bufs=2))
        work = ctx.enter_context(tc.tile_pool(name="work", bufs=2))
        psum_s = ctx.enter_context(tc.psum_pool(name="psum_s", bufs=BANKS))
        psum_l = ctx.enter_context(tc.psum_pool(name="psum_l", bufs=2))
        psum_o = ctx.enter_context(tc.psum_pool(name="psum_o", bufs=1))
        ctx.enter_context(tc.manual_schedule())

        rows_of = {}

        def load(h, pieces):
            k_rows = rows.tile([P, N_BLOCKS, PACK, HEAD_DIM], BF16)
            q_rows = rows.tile([P, N_BLOCKS, TILES_PER_BLOCK, HEAD_DIM], BF16)
            v_rows = rows.tile([P, N_BLOCKS, PACK, HEAD_DIM], BF16)
            k_src = k[0, h].rearrange("(g p t) d -> p g t d", p=P, t=PACK)
            v_src = v[0, h].rearrange("(g p t) d -> p g t d", p=P, t=PACK)
            q_src = q[0, h].rearrange("(b r p) d -> p b r d", p=P, r=TILES_PER_BLOCK)
            for which, lo, hi in pieces:
                rows_tile, src = {"k": (k_rows, k_src), "q": (q_rows, q_src), "v": (v_rows, v_src)}[which]
                nc.sync.dma_start(out=rows_tile[:, lo:hi], in_=src[:, lo:hi])
            rows_of[h] = (k_rows, q_rows, v_rows)

        whole = [("k", 0, N_BLOCKS), ("q", 0, N_BLOCKS), ("v", 0, N_BLOCKS)]
        slope_row = const.tile([P, HEADS], BF16)
        nc.vector.memset(slope_row[:], 0.0)
        nc.sync.dma_start(out=slope_row[0:1], in_=log_slope.rearrange("(a h) -> a h", a=1))
        load(0, [("k", 0, 1), ("q", 1, 2), ("k", 1, 2), ("q", 0, 1), ("q", 2, 4), ("k", 2, 4), ("v", 0, 4)])
        warm = const.tile([P, 1], F32)
        nc.vector.memset(warm[:], 0.0)
        warmed = const.tile([P, 1], F32)
        nc.scalar.activation(out=warmed[:], in_=warm[:], func=ACT.Exp)
        ones = const.tile([P, P], BF16)
        nc.vector.memset(ones[:], 1.0)

        dist_int = const.tile([P, P, PACK], I32)
        nc.gpsimd.iota(dist_int[:], pattern=[[1, P], [-1, PACK]], base=LAST * P, channel_multiplier=-PACK)
        step_int = const.tile([P, FAR_STEPS], I32)
        nc.gpsimd.iota(step_int[:], pattern=[[P, FAR_STEPS]], base=0, channel_multiplier=0)
        ident = const.tile([P, P], BF16)
        make_identity(nc, ident[:])

        k_even_a = const.tile([P, N_PAIRS, PACK, LAST * STEP + P], BF16, align_bytes=64)
        k_even_b = const.tile([P, N_PAIRS, PACK, LAST * STEP + P], BF16, align_bytes=64)
        k_part_a = const.tile([P, LAST, N_PAIRS, PACK, P], BF16, align_bytes=64)
        k_part_b = const.tile([P, LAST, N_PAIRS, PACK, P], BF16, align_bytes=64)
        v_part_a = const.tile([P, 2, LAST, N_PAIRS, HEAD_DIM], U32, align_bytes=64)
        v_part_b = const.tile([P, 2, LAST, N_PAIRS, HEAD_DIM], U32, align_bytes=64)
        vs_part_a = const.tile([P, LAST, N_PAIRS, HEAD_DIM], U8, align_bytes=64)
        vs_part_b = const.tile([P, LAST, N_PAIRS, HEAD_DIM], U8, align_bytes=64)
        v_scales_a = const.tile([P, N_BLOCKS, HEAD_DIM], U8, align_bytes=64)
        v_scales_b = const.tile([P, N_BLOCKS, HEAD_DIM], U8, align_bytes=64)
        k_even = [k_even_a, k_even_b]
        k_part = [k_part_a, k_part_b]
        v_part = [v_part_a, v_part_b]
        vs_part = [vs_part_a, vs_part_b]
        v_scales = [v_scales_a, v_scales_b]

        def zero_set(i):
            nc.gpsimd.memset(k_even[i][:].bitcast(U32)[:, :, :, 0 : LAST * STEP // 2], 0)
            for r in range(LAST):
                nc.gpsimd.memset(k_part[i][:].bitcast(U32)[:, r, :, :, (r + 1) * STEP // 2 : P // 2], 0)
            nc.gpsimd.memset(v_part[i][:], 0)
            nc.gpsimd.memset(vs_part[i][:].bitcast(U32), 0)
            nc.gpsimd.memset(v_scales[i][:].bitcast(U32), 0)

        zero_set(0)
        zero_set(1)

        l_bank = psum_l.tile([P, HEADS], F32)
        nc.tensor.matmul(l_bank[:], lhsT=ones[:], rhs=slope_row[:], start=True, stop=True)
        slope = const.tile([P, HEADS], F32)
        dist = const.tile([P, P, PACK], F32)
        nc.vector.tensor_copy(out=dist[:], in_=dist_int[:])
        step = const.tile([P, FAR_STEPS], F32)
        nc.vector.tensor_copy(out=step[:], in_=step_int[:])
        causal = const.tile([P, P, PACK], F32)
        nc.vector.scalar_tensor_tensor(
            out=causal[:], in0=dist[:], scalar=-FOREVER, in1=dist[:], op0=ALU.mult, op1=ALU.max
        )
        pack_0 = const.tile([P, P, PACK], F32)
        pack_1 = const.tile([P, P, PACK], F32)
        pack_2 = const.tile([P, P, PACK], F32)
        own_dist = [pack_0, pack_1, pack_2, causal]
        nc.vector.tensor_scalar_min(out=slope[:], in0=l_bank[:], scalar1=-TINY)
        slope_tile = const.tile([P, HEADS], F32)
        nc.vector.tensor_scalar_mul(out=slope_tile[:], in0=slope[:], scalar1=float(P))
        q_cols_of = {}
        k_odd_of = {}
        table_of = {}
        far_step_of = {}
        v_grouped_of = {}
        v_codes_of = {}

        def flip(row_tiles, early=0):
            n_tiles = PACK * len(row_tiles)
            if early == 1:
                s_bank = psum_s.tile([P, n_tiles, P], BF16)
                flipped = s_bank
            elif early == 2:
                l_bank = psum_l.tile([P, n_tiles, P], BF16)
                flipped = l_bank
            else:
                o_bank = psum_o.tile([P, n_tiles, P], BF16)
                flipped = o_bank
            for i, tiles in enumerate(row_tiles):
                for j in range(PACK):
                    nc.tensor.transpose(flipped[:, i * PACK + j, :], tiles[:, j, :], ident[:])
            return flipped

        def flip_q(h, blocks, early=0, by_vector=False):
            if h not in q_cols_of:
                q_cols = head.tile([P, N_BLOCKS * TILES_PER_BLOCK, P], BF16)
                q_cols_of[h] = q_cols
            flipped = flip([rows_of[h][1][:, b] for b in blocks], early)
            first = blocks[0] * TILES_PER_BLOCK
            dst = q_cols_of[h][:, first : first + TILES_PER_BLOCK * len(blocks)]
            if by_vector:
                nc.vector.tensor_copy(out=dst, in_=flipped[:])
            else:
                nc.scalar.copy(out=dst, in_=flipped[:])

        def flip_k(h, groups, early=0):
            if h not in k_odd_of:
                k_odd = head.tile([P, N_PAIRS, PACK, P], BF16, align_bytes=64)
                k_odd_of[h] = k_odd
            flipped = flip([rows_of[h][0][:, g] for g in groups], early)
            for i, g in enumerate(groups):
                src = flipped[:, i * PACK : (i + 1) * PACK, :]
                if g % 2 == 0:
                    dst = k_even[h % 2][:, g // 2, :, LAST * STEP :]
                else:
                    dst = k_odd_of[h][:, g // 2]
                if early == 1:
                    nc.vector.tensor_copy(out=dst, in_=src)
                else:
                    nc.scalar.copy(out=dst, in_=src)
                if g % 2 == 1:
                    for r in range(LAST):
                        nc.sync.dma_start(
                            out=k_part[h % 2][:, r, g // 2, :, 0 : (r + 1) * STEP],
                            in_=k_odd_of[h][:, g // 2, :, 0 : (r + 1) * STEP],
                        )

        def decay_far(h):
            slope_h = slope[:, h : h + 1]
            far = head.tile([P, P, PACK], F32)
            nc.scalar.activation(
                out=far[:], in_=dist[:], func=ACT.Exp, bias=slope_tile[:, h : h + 1], scale=slope_h
            )
            table_of[(h, "far")] = far
            far_step = head.tile([P, FAR_STEPS], F32)
            nc.scalar.activation(out=far_step[:], in_=step[:], func=ACT.Exp, scale=slope_h)
            far_step_of[h] = far_step

        def decay_own(h, r):
            own = head.tile([P, P, PACK], F32, bufs=2 * TILES_PER_BLOCK)
            nc.scalar.activation(out=own[:], in_=own_dist[r][:], func=ACT.Exp, scale=slope[:, h : h + 1])
            table_of[(h, r)] = own

        def regroup_v(h, g):
            if g == 0:
                v_grouped = head.tile([P, N_BLOCKS, HEAD_DIM, PACK], BF16, align_bytes=64)
                v_grouped_of[h] = v_grouped
            src = rows_of[h][2][:, g].rearrange("p t d -> p d t")
            nc.scalar.copy(out=v_grouped_of[h][:, g], in_=src)

        def quantise_v(h):
            v_codes = head.tile([P, N_BLOCKS, HEAD_DIM], U32, align_bytes=64)
            nc.vector.quantize_mx(
                out=v_codes[:].rearrange("p g d -> p (g d)").bitcast(FP8X4),
                scales=v_scales[h % 2][:].rearrange("p g d -> p (g d)"),
                in_=v_grouped_of[h][:].rearrange("p g d t -> p (g d t)"),
            )
            v_codes_of[h] = v_codes

        def spread_v(h):
            v_codes = v_codes_of[h]
            for r in range(LAST):
                live = (r + 1) * STEP
                for at, n in pieces(live):
                    src = slice(at, at + n)
                    high = slice(P - live + at, P - live + at + n)
                    words = v_codes[src].rearrange("p (j e) d -> p e j d", e=2)
                    scales = v_scales[h % 2][src].rearrange("p (j e) d -> p e j d", e=2)
                    nc.sync.dma_start(out=v_part[h % 2][high, 0, r].bitcast(I32), in_=words[:, 0].bitcast(I32))
                    nc.sync.dma_start(out=vs_part[h % 2][high, r].bitcast(I32), in_=scales[:, 0].bitcast(I32))
                    nc.sync.dma_start(out=v_part[h % 2][src, 1, r].bitcast(I32), in_=words[:, 1].bitcast(I32))

        halves = [(h, i) for h in range(HEADS) for i in range(2)]
        phases = []
        direct_tiles = []
        helped_tiles = []
        place = {}
        ends_of = []
        for h, i in halves:
            kind = ("opening" if h == 0 else "first") if i == 0 else "second" if h + 1 < HEADS else "closing"
            tiles = {"opening": OPENING, "first": FIRST, "second": SECOND, "closing": CLOSING}[kind]
            direct = [tile for tile in tiles if tile not in HELPED[kind]]
            helped = list(HELPED[kind])
            phase_ends = []
            done = 0
            for n_direct, n_helped in PHASES[kind]:
                p = len(phases)
                done += n_direct
                phase_ends.append((done, p))
                phases.append((len(direct_tiles), len(helped_tiles), n_direct, n_helped))
                for j in range(n_direct + n_helped):
                    if j < n_direct:
                        tile = direct[j]
                        direct_tiles.append((p, j, h, tile))
                    else:
                        tile = helped[j - n_direct]
                        helped_tiles.append((p, j - n_direct, h, tile))
                    place[(h, tile)] = (p, j)
                direct = direct[n_direct:]
                helped = helped[n_helped:]
            ends_of.append(phase_ends)

        def product(bank, h, tile):
            def k_cols(g, t):
                if g % 2 == 0:
                    return k_even[h % 2][:, g // 2, t, LAST * STEP :]
                return k_odd_of[h][:, g // 2, t]

            q_cols = q_cols_of[h]
            if tile[0] == "pack":
                kind, j, r = tile
                for t in range(PACK):
                    nc.tensor.matmul(
                        bank[:, t, :],
                        lhsT=k_even[h % 2][:, j, t, r * STEP : r * STEP + P],
                        rhs=q_cols[:, 2 * j * TILES_PER_BLOCK + r],
                        start=True,
                        stop=False,
                    )
                    nc.tensor.matmul(
                        bank[:, t, :],
                        lhsT=k_part[h % 2][:, LAST - 1 - r, j, t],
                        rhs=q_cols[:, (2 * j + 1) * TILES_PER_BLOCK + LAST - 1 - r],
                        start=False,
                        stop=True,
                    )
            else:
                b = tile[1]
                g, r = (b, LAST) if tile[0] == "near" else tile[2:]
                for t in range(PACK):
                    nc.tensor.matmul(bank[:, t, :], lhsT=k_cols(g, t), rhs=q_cols[:, b * TILES_PER_BLOCK + r], start=True, stop=True)

        def far_scalar(h, tile):
            kind, b, g, r = tile
            s = (b - g - 1) * TILES_PER_BLOCK + r
            return far_step_of[h][:, s : s + 1]

        def table(h, tile):
            if tile[0] == "far":
                return table_of[(h, "far")]
            return table_of[(h, LAST if tile[0] == "near" else tile[2])]

        bank_of = {}
        energy_of = {}
        helped_of = {}
        lifted_of = {}
        codes_of = {}

        def fill(n):
            p, slot, h, tile = direct_tiles[n]
            s_bank = psum_s.tile([P, PACK, P], F32)
            product(s_bank, h, tile)
            bank_of[n] = s_bank


        def multiply(n):
            p, slot, h, tile = direct_tiles[n]
            if p not in energy_of:
                energy = work.tile([P, phases[p][2], P, PACK], BF16, align_bytes=64)
                energy_of[p] = energy
            s_view = bank_of[n][:].rearrange("p t c -> p c t")
            dst = energy_of[p][:, slot]
            if tile[0] == "far":
                nc.vector.scalar_tensor_tensor(
                    out=dst, in0=s_view, scalar=far_scalar(h, tile), in1=table(h, tile)[:], op0=ALU.mult, op1=ALU.mult
                )
            else:
                nc.vector.tensor_tensor(out=dst, in0=s_view, in1=table(h, tile)[:], op=ALU.mult)

        def lift(m):
            p, at, h, tile = helped_tiles[m]
            if at == 0:
                lifted = work.tile([P, phases[p][3], P, PACK], F32, bufs=LIFT_BUFS)
                lifted_of[p] = lifted
            l_bank = psum_l.tile([P, PACK, P], F32)
            product(l_bank, h, tile)
            nc.scalar.activation(
                out=lifted_of[p][:, at],
                in_=l_bank[:].rearrange("p t c -> p c t"),
                func=ACT.Copy,
                scale=far_scalar(h, tile),
            )

        def help_phase(p):
            m, n_helped = phases[p][1], phases[p][3]
            h = helped_tiles[m][2]
            helped = work.tile([P, n_helped, P * PACK], BF16, align_bytes=64, bufs=1)
            nc.gpsimd.tensor_tensor(
                out=helped[:],
                in0=lifted_of[p][:].rearrange("p s c t -> p s (c t)"),
                in1=table_of[(h, "far")][:].rearrange("p c t -> p (c t)").unsqueeze(1).to_broadcast([P, n_helped, P * PACK]),
                op=ALU.mult,
            )
            helped_of[p] = helped

        def quantise(p, source, base):
            if p not in codes_of:
                e_codes = work.tile([P, WIDEST, P], U32, align_bytes=64, bufs=CODE_BUFS)
                e_scales = work.tile([P, WIDEST, P], U8, align_bytes=64, bufs=CODE_BUFS)
                codes_of[p] = (e_codes, e_scales)
            e_codes, e_scales = codes_of[p]
            for at, w in widths(source.shape[1]):
                slots = slice(base + at, base + at + w)
                nc.vector.quantize_mx(
                    out=e_codes[:, slots].rearrange("p s c -> p (s c)").bitcast(FP8X4),
                    scales=e_scales[:, slots].rearrange("p s c -> p (s c)"),
                    in_=source[:, at : at + w].rearrange("p s e -> p (s e)"),
                )

        def quantise_phase(p):
            quantise(p, energy_of[p][:].rearrange("p s c t -> p s (c t)"), 0)
            quantise(p, helped_of[p][:], phases[p][2])

        o_bank_of = {}

        def second_matmul(h, b, r):
            if h == HEADS - 1 and b == N_BLOCKS - 1:
                s_bank = psum_s.tile([P, TILES_PER_BLOCK, HEAD_DIM], F32)
                o_bank_of[(h, b)] = s_bank
            elif h == HEADS - 1 and b == N_BLOCKS - 2 and r == 0:
                l_bank = psum_l.tile([P, TILES_PER_BLOCK, HEAD_DIM], F32)
                o_bank_of[(h, b)] = l_bank
            elif (h, b) not in o_bank_of:
                o_bank = psum_o.tile([P, TILES_PER_BLOCK, HEAD_DIM], F32)
                o_bank_of[(h, b)] = o_bank
            passes = []
            for g in range(b):
                passes.append((("far", b, g, r), v_codes_of[h][:, g], v_scales[h % 2][:, g]))
            j, odd = b // 2, b % 2
            if r == LAST:
                passes.append((("near", b), v_codes_of[h][:, b], v_scales[h % 2][:, b]))
            elif odd:
                passes.append((("pack", j, LAST - 1 - r), v_part[h % 2][:, 1, r, j], v_scales[h % 2][:, b]))
            else:
                passes.append((("pack", j, r), v_part[h % 2][:, 0, r, j], vs_part[h % 2][:, r, j]))
            for i, (tile, v_words, v_sc) in enumerate(passes):
                p, slot = place[(h, tile)]
                e_codes, e_scales = codes_of[p]
                nc.tensor.matmul_mx(
                    out=o_bank_of[(h, b)][:, r, :],
                    lhsT=e_codes[:, slot].bitcast(FP8X4),
                    lhsT_scale=e_scales[:, slot],
                    rhs=v_words.bitcast(FP8X4),
                    rhs_scale=v_sc,
                    start=(i == 0),
                    stop=(i == len(passes) - 1),
                )

        def store(h, b, first, last, by_vector=False):
            if first == 0:
                o_rows = work.tile([P, TILES_PER_BLOCK, HEAD_DIM], F32, bufs=3)
                o_rows_of[(h, b)] = o_rows
            o_rows = o_rows_of[(h, b)]
            src = o_bank_of[(h, b)][:, first:last]
            if by_vector:
                nc.vector.tensor_copy(out=o_rows[:, first:last], in_=src)
            else:
                nc.scalar.copy(out=o_rows[:, first:last], in_=src)
            nc.sync.dma_start(
                out=out[0, h, b * BLOCK + first * P : b * BLOCK + last * P, :].rearrange("(r p) d -> p r d", p=P),
                in_=o_rows[:, first:last],
            )

        o_rows_of = {}

        def block_step(h, b, r):
            second_matmul(h, b, r)
            if r == LAST:
                store(h, b, 0, TILES_PER_BLOCK)

        def chore(c, s):
            h, i = halves[c]
            if h == 0 and s == FIRST_LOADS[i]:
                load(1 + i, whole)
            if 0 < h < HEADS - 2 and i == 1 and s == LOAD_AT:
                load(h + 2, whole)
            due = [(h - 1, 2 * i + b, at) for b, at in enumerate(OUT_AT[i])] if h > 0 else []
            if c + 1 == len(halves):
                due += [(h, b, at) for b, at in enumerate(OUT_CLOSE)]
            for of, b, at in due:
                if s == at:
                    for r in range(TILES_PER_BLOCK):
                        second_matmul(of, b, r)
                    store(of, b, 0, TILES_PER_BLOCK)
            for at, what, which in OWN_0[i] if h == 0 else OWN[i]:
                if s == at:
                    what_of[what](h, which)
            if h + 1 < HEADS:
                for at, what, which in NEXT_0[i] if h == 0 else NEXT[i]:
                    if s == at:
                        what_of[what](h + 1, which)

        what_of = {
            "k": flip_k,
            "q": flip_q,
            "v": regroup_v,
            "far": lambda h, which: decay_far(h),
            "own": decay_own,
        }

        flip_k(0, (0,), 1)
        decay_far(0)
        flip_q(0, (1,), 2)
        flip_k(0, (1,), 1)
        flip_q(0, (0,), by_vector=True)
        decay_own(0, LAST)
        for r in range(LAST):
            low = (LAST - r) * STEP
            for at, n in pieces(P - low):
                nc.sync.dma_start(out=own_dist[r][low + at : low + at + n], in_=causal[low + at : low + at + n])
            for at, n in pieces(low):
                nc.sync.dma_start(out=own_dist[r][at : at + n], in_=causal[P - low + at : P - low + at + n])
        fill(0)
        fill(1)
        fill(2)
        fill(3)
        fill(4)
        lift(0)
        flip_q(0, (2, 3), 2)
        order = []
        for first, helped_first, n_direct, n_helped in phases:
            at = first + (min(BANKS, n_direct) - 1 if first > 0 else 1)
            rest = [m for m in range(first + 1, first + n_direct) if m != at]
            if first > 0:
                tail = rest[BANKS - 2 :]
                rest = rest[: BANKS - 2] + [m for i in range(0, len(tail), 2) for m in reversed(tail[i : i + 2])]
            order += [first, at] + rest
        multiplied = set()
        n_filled = BANKS
        n = 0
        turn = None
        for c in range(len(halves)):
            h, i = halves[c]
            closing = c + 1 == len(halves)
            lift_at = LIFT_AT[i] if h > 0 else (LIFT_0, LIFT_1)[i]
            n_steps = ends_of[c][-1][0]
            first_lift = phases[ends_of[c][-1][1]][1] + phases[ends_of[c][-1][1]][3]
            for s in range(n_steps):
                multiply(order[n])
                multiplied.add(order[n])
                if turn is not None:
                    if turn[1] is not None:
                        quantise_v(turn[1])
                        spread_v(turn[1])
                    quantise_phase(turn[0])
                    help_phase(turn[0] + 1)
                    turn = None
                while n_filled < len(direct_tiles) and n_filled - BANKS in multiplied:
                    fill(n_filled)
                    n_filled += 1
                if c == 0:
                    if s in START_LIFT:
                        m = 1 + START_LIFT.index(s)
                        lift(m)
                        if m + 1 == PHASES["opening"][0][1]:
                            help_phase(0)
                    for at, what, which in START_PREP:
                        if s == at:
                            what_of[what](0, which)
                if not closing:
                    for j in range(HELP):
                        if s == lift_at[j]:
                            lift(first_lift + j)
                chore(c, s)
                if closing and s >= n_steps - TILES_PER_BLOCK:
                    second_matmul(HEADS - 1, 2, s - n_steps + TILES_PER_BLOCK)
                    if s == n_steps - 1:
                        store(HEADS - 1, 2, 0, TILES_PER_BLOCK)
                n += 1
                for end, p in ends_of[c]:
                    if s + 1 == end:
                        packing = None
                        if (end == n_steps and i == 0 and h > 0) or (end < n_steps and c == 1):
                            packing = h
                        turn = (p, packing)
            if closing:
                for r in range(2):
                    second_matmul(HEADS - 1, 3, r)
                    store(HEADS - 1, 3, r, r + 1)
                break
        last = len(phases) - 1
        quantise(last, helped_of[last][:], phases[last][2])
        quantise(last, energy_of[last][:].rearrange("p s c t -> p s (c t)"), 0)
        for r in (2, LAST):
            second_matmul(HEADS - 1, 3, r)
            store(HEADS - 1, 3, r, r + 1, by_vector=(r == LAST))
